import numpy as np
import ml_dtypes


def mxq(x, axis, fmt="e4m3"):
    dtype, down = {"e4m3": (ml_dtypes.float8_e4m3fn, 7), "e5m2": (ml_dtypes.float8_e5m2, 14)}[fmt]
    v = np.moveaxis(np.asarray(x, np.float32).astype(ml_dtypes.bfloat16).astype(np.float64), axis, -1)
    blocks = v.reshape(v.shape[:-1] + (-1, 32))
    amax = np.abs(blocks).max(-1, keepdims=True)
    byte = np.maximum(np.where(amax > 0, np.frexp(amax)[1] - 1 + 127, 0) - down, 1)
    scale = np.exp2(byte - 127.0)
    codes = (blocks / scale).astype(np.float32).astype(dtype).astype(np.float64)
    return np.moveaxis((codes * scale).reshape(v.shape), -1, axis)


WIDE = False


def mx_kscale(k):
    if not WIDE:
        return np.ones(k)
    levels = np.array([10, -10, 5, -5, 0])
    a = np.random.permutation(np.resize(levels, k // 512 * 4)).reshape(k // 512, 4)
    idx = np.arange(k)
    return np.exp2(a[idx // 512, idx % 128 // 32])


BF16 = ml_dtypes.bfloat16


def bf(x):
    return np.asarray(x, np.float32).astype(BF16)


def f64(x):
    return np.asarray(x).astype(np.float64)


M, DI, N, DO, TS = 4096, 512, 512, 1024, 3
DENSITY = 0.25


def setup_inputs():
    k = mx_kscale(DI)
    m = (np.random.uniform(size=(N, N)) < DENSITY).astype(np.float64)
    return {'x': bf(np.random.standard_normal((M, DI)) * k),
            'W_in': bf(np.random.standard_normal((N, DI)) / np.sqrt(DI) / k),
            'b_in': bf(np.random.standard_normal(N) * 0.3),
            'weights': bf(np.random.standard_normal((N, N)) * 1.5 / np.sqrt(DENSITY * N)),
            'J': bf(np.random.standard_normal((N, N)) * 2.0 / np.sqrt(DENSITY * N)),
            'theta': bf(np.random.uniform(size=N) * 1.0 + 0.25),
            'lam': bf(0.35 + 0.05 * np.random.standard_normal(1)),
            'mask': bf(m * (1.0 - np.eye(N))),
            'noise_raw': bf(np.random.standard_normal((M, N)) * 2.5)}


def reference(x, W_in, b_in, weights, J, theta, lam, mask, noise_raw):
    state = (mxq(f64(x), 1, 'e4m3') @ mxq(f64(W_in), 1, 'e4m3').T) + f64(b_in)
    eff_w = f64(weights) * f64(mask)
    J_m = f64(J) * f64(mask)
    T = np.abs(np.sin(2.0 * f64(theta)))
    signal = mxq(state, 1, 'e4m3') @ mxq(eff_w, 0, 'e4m3')
    s = np.tanh(state)
    delta = (mxq(s, 1, 'e4m3') @ mxq(J_m, 0, 'e4m3')) * s
    noise = f64(noise_raw) * T * 0.1
    return np.tanh(signal + f64(lam) * delta + noise)

@@ -1,0 +1,257 @@
+from contextlib import ExitStack
+import math
+
+import concourse.mybir as mybir
+from concourse.masks import make_identity
+
+F32 = mybir.dt.float32
+BF16 = mybir.dt.bfloat16
+U32 = mybir.dt.uint32
+U8 = mybir.dt.uint8
+I32 = mybir.dt.int32
+FP8X4 = mybir.dt.float8_e4m3fn_x4
+ACT = mybir.ActivationFunctionType
+ALU = mybir.AluOpType
+
+P = 128
+M, D = 4096, 512
+CH = 512
+NCH = M // CH
+FLOPS = 3 * 2 * M * D * D
+
+PI_HI = 3.1415927410125732
+PI_LO = math.pi - PI_HI
+
+PRO = [("WPREP", 0, -1, ""), ("XX", 0, 0, "S"), ("XX", 0, 1, "V"), ("QX", 0, -1, ""), ("PP", 0, 2, "V"), ("PP", 0, 0, "S"), ("XX", 1, 0, "S"), ("MK", 0, 0, "V"), ("XX", 1, 1, "V"), ("MK", 0, 1, "G"), ("PP", 0, 1, "V"), ("QX", 1, -1, ""), ("QM", 0, 0, ""), ("QM", 0, 1, ""), ("PP", 0, 3, "S"), ("PP", 1, 0, "S"), ("RG2", 0, -1, "V"), ("PP", 1, 1, "S"), ("QT", 0, -1, ""), ("PP", 1, 2, "S"), ("DP", 0, 0, ""), ("RG1", 0, -1, "G"), ("NT", 0, 0, ""), ("QS", 0, -1, ""), ("PP", 1, 3, "S"), ("SG", 0, 0, "")]
+BODY = [("A", 0, 0, ""), ("DP", 0, 1, ""), ("XX", 2, 0, ""), ("XX", 2, 1, ""), ("B", 0, 0, ""), ("NT", 0, 1, ""), ("NT", 1, 0, ""), ("FP", -1, 0, ""), ("FP", -1, 1, ""), ("FP", -1, 2, ""), ("FP", -1, 3, ""), ("ST", -1, -1, ""), ("C", 0, 0, ""), ("SG", 0, 1, ""), ("A", 0, 1, ""), ("QX", 2, -1, ""), ("PP", 2, 0, ""), ("PP", 2, 1, ""), ("RG2", 1, -1, ""), ("QT", 1, -1, ""), ("DP", 1, 0, ""), ("B", 0, 1, ""), ("PP", 2, 2, ""), ("PP", 2, 3, ""), ("C", 0, 1, ""), ("RG1", 1, -1, ""), ("QS", 1, -1, ""), ("SG", 1, 0, "")]
+EPI = [("FP", 0, 0, ""), ("FP", 0, 1, ""), ("FP", 0, 2, ""), ("FP", 0, 3, ""), ("ST", 0, -1, "")]
+
+
+def tile_brainquantumlayer_pa_t_kernel(tc, x, W_in, b_in, weights, J, theta, lam, mask, noise_raw, out):
+    nc = tc.nc
+    with ExitStack() as ctx:
+        ctx.enter_context(tc.manual_schedule())
+        keep = ctx.enter_context(tc.tile_pool(name="keep", bufs=1))
+        work = ctx.enter_context(tc.tile_pool(name="work", bufs=2))
+        psum = ctx.enter_context(tc.psum_pool(name="psum", bufs=2))
+
+        x_v = x.rearrange("(c p s) k -> c p s k", p=P, s=4)
+        n_v = noise_raw.rearrange("(c p s) k -> c p s k", p=P, s=4)
+        o_v = out.rearrange("(c p s) k -> c p s k", p=P, s=4)
+
+        def load_upe(dst, w):
+            nc.sync.dma_start(out=dst[:].rearrange("p (u e) j -> p u (e j)", u=2),
+                              in_=w.rearrange("(u p e) j -> p u (e j)", u=2, p=P, e=2))
+
+        b_bf = keep.tile([P, 4], BF16, name="b_bf")
+        th_bf = keep.tile([P, 4], BF16, name="th_bf")
+        lam_bf = keep.tile([P, 1], BF16, name="lam_bf")
+        with nc.allow_non_contiguous_dma(reason="three small vectors, once"):
+            nc.scalar.dma_start(out=th_bf[:].rearrange("p (u e) -> p u e", u=2), in_=theta.rearrange("(u p e) -> p u e", u=2, p=P, e=2))
+            nc.scalar.dma_start(out=b_bf[:].rearrange("p (u e) -> p u e", u=2), in_=b_in.rearrange("(u p e) -> p u e", u=2, p=P, e=2))
+            nc.scalar.dma_start(out=lam_bf[:], in_=lam.partition_broadcast(P))
+
+        w_in_sb = keep.tile([P, 4, D], BF16, name="w_in_sb")
+        load_upe(w_in_sb, W_in)
+        x_sb = []
+        n_sb = []
+        for c in range(NCH):
+            x_sb.append(keep.tile([P, 4, D], BF16, name="x_sb%d" % c))
+            n_sb.append(keep.tile([P, 4, D], BF16, name="n_sb%d" % c))
+        nc.sync.dma_start(out=x_sb[0][:], in_=x_v[0])
+        w_sb = keep.tile([P, 4, D], BF16, name="w_sb")
+        m_sb = keep.tile([P, 4, D], BF16, name="m_sb")
+        j_sb = keep.tile([P, 4, D], BF16, name="j_sb")
+        load_upe(j_sb, J)
+        load_upe(m_sb, mask)
+        load_upe(w_sb, weights)
+        for c in range(NCH):
+            if c + 1 < NCH:
+                nc.sync.dma_start(out=x_sb[c + 1][:], in_=x_v[c + 1])
+            nc.sync.dma_start(out=n_sb[c][:], in_=n_v[c])
+
+        ident = keep.tile([P, P], F32, name="ident")
+        make_identity(nc, ident[:])
+
+        th2 = keep.tile([P, 4], F32, name="th2")
+        nc.vector.tensor_scalar_mul(out=th2[:], in0=th_bf[:], scalar1=2.0)
+        kq = keep.tile([P, 4], F32, name="kq")
+        nc.vector.tensor_scalar_mul(out=kq[:], in0=th_bf[:], scalar1=2.0 / math.pi)
+        ki = keep.tile([P, 4], I32, name="ki")
+        nc.vector.tensor_copy(out=ki[:], in_=kq[:])
+        kf = keep.tile([P, 4], F32, name="kf")
+        nc.vector.tensor_copy(out=kf[:], in_=ki[:])
+        y1 = keep.tile([P, 4], F32, name="y1")
+        nc.vector.scalar_tensor_tensor(out=y1[:], in0=kf[:], scalar=-PI_HI, in1=th2[:], op0=ALU.mult, op1=ALU.add)
+        y2 = keep.tile([P, 4], F32, name="y2")
+        nc.vector.scalar_tensor_tensor(out=y2[:], in0=kf[:], scalar=-PI_LO, in1=y1[:], op0=ALU.mult, op1=ALU.add)
+        sn = keep.tile([P, 4], F32, name="sn")
+        nc.scalar.activation(out=sn[:], in_=y2[:], func=ACT.Sin)
+        t01 = keep.tile([P, 4], F32, name="t01")
+        nc.scalar.activation(out=t01[:], in_=sn[:], func=ACT.Abs, scale=0.1)
+        b_f = keep.tile([P, 4], F32, name="b_f")
+        nc.vector.tensor_copy(out=b_f[:], in_=b_bf[:])
+        lam_f = keep.tile([P, 1], F32, name="lam_f")
+        nc.vector.tensor_copy(out=lam_f[:], in_=lam_bf[:])
+
+        st = {}
+
+        def grp_tile():
+            return work.tile([P, 4 * D], BF16, name="grp", tag="grp", bufs=3, align_bytes=64)
+
+        def t_bank(rows, h):
+            bank = psum.tile([P, 2, 256], F32, name="bank_t", tag="wk", bufs=2)
+            for i in range(2):
+                src = rows(2 * h + i).bitcast(F32)
+                for v in range(2):
+                    nc.tensor.transpose(out=bank[:, v, P * i:P * (i + 1)], in_=src[:, P * v:P * (v + 1)], identity=ident[:])
+            return bank
+
+        def evac(bank, grouped, h, eng):
+            dst = grouped[:].bitcast(F32).rearrange("p (m v) -> p m v", v=2)[:, 256 * h:256 * (h + 1), :]
+            src = bank[:].rearrange("p v m -> p m v")
+            if eng == "V":
+                nc.vector.tensor_copy(out=dst, in_=src)
+            else:
+                nc.scalar.copy(out=dst, in_=src)
+
+        def quantise(grouped, name, bufs):
+            pool = keep if bufs == 1 else work
+            codes = pool.tile([P, D], U32, name=name + "_c", bufs=bufs, align_bytes=64)
+            scales = pool.tile([P, D], U8, name=name + "_s", bufs=bufs, align_bytes=64)
+            nc.vector.quantize_mx(out=codes[:].bitcast(FP8X4), scales=scales[:], in_=grouped[:])
+            return codes, scales
+
+        def mx(acc, lhs, t, rhs):
+            cols = slice(P * t, P * (t + 1))
+            nc.tensor.matmul_mx(out=acc, lhsT=lhs[0][:, cols].bitcast(FP8X4), lhsT_scale=lhs[1][:, cols],
+                                rhs=rhs[0][:].bitcast(FP8X4), rhs_scale=rhs[1][:], start=True, stop=True)
+
+        def regroup(dst, src, eng):
+            if eng == "V":
+                nc.vector.tensor_copy(out=dst[:].rearrange("p (c i t) -> p c t i", i=4, t=4),
+                                      in_=src[:].rearrange("p t (c i) -> p c t i", i=4))
+            else:
+                nc.gpsimd.tensor_scalar(out=dst[:].rearrange("p (m t) -> p m t", t=4), in0=src[:].rearrange("p t m -> p m t"),
+                                        scalar1=1.0, scalar2=0.0, op0=ALU.mult, op1=ALU.add)
+
+        def WPREP(c, a, eng):
+            wg = grp_tile()
+            for h in range(2):
+                bank = t_bank(lambda i: w_in_sb[:, i, :], h)
+                evac(bank, wg, h, "V" if h == 0 else "S")
+            st["wq"] = quantise(wg, "w_q", 1)
+
+        def MK(c, a, eng):
+            g = grp_tile()
+            w = j_sb if a == 0 else w_sb
+            gv = g[:].rearrange("p (u e q t) -> p u e q t", u=2, e=2, q=P, t=4)
+            wv = w[:].rearrange("p t (u q e) -> p u e q t", u=2, q=P, e=2)
+            mv = m_sb[:].rearrange("p t (u q e) -> p u e q t", u=2, q=P, e=2)
+            for e in range(2):
+                if eng == "G":
+                    nc.gpsimd.tensor_tensor(out=gv[:, :, e, :, :], in0=wv[:, :, e, :, :], in1=mv[:, :, e, :, :], op=ALU.mult)
+                else:
+                    nc.vector.tensor_tensor(out=gv[:, :, e, :, :], in0=wv[:, :, e, :, :], in1=mv[:, :, e, :, :], op=ALU.mult)
+            st["mg", a] = g
+
+        def QM(c, a, eng):
+            st["mq", a] = quantise(st["mg", a], "m_q%d" % a, 1)
+
+        def XX(c, h, eng):
+            if h == 0:
+                st["xg", c] = grp_tile()
+            bank = t_bank(lambda i: x_sb[c][:, i, :], h)
+            evac(bank, st["xg", c], h, eng)
+
+        def QX(c, a, eng):
+            st["xq", c] = quantise(st["xg", c], "x_q", 2)
+
+        def PP(c, t, eng):
+            if ("pl", c) not in st:
+                st["pl", c] = work.tile([P, 4, CH], BF16, name="pl", bufs=2)
+                st["sT", c] = work.tile([P, 4, CH], F32, name="sT", bufs=3)
+            acc = psum.tile([P, CH], F32, name="acc_st", tag="wk", bufs=2)
+            mx(acc[:], st["wq"], t, st["xq", c])
+            if eng == "V":
+                nc.vector.tensor_scalar_add(out=st["pl", c][:, t, :], in0=acc[:], scalar1=b_f[:, t:t + 1])
+            else:
+                nc.scalar.activation(out=st["pl", c][:, t, :], in_=acc[:], func=ACT.Identity, bias=b_f[:, t:t + 1], scale=1.0)
+            nc.scalar.activation(out=st["sT", c][:, t, :], in_=acc[:], func=ACT.Tanh, bias=b_f[:, t:t + 1], scale=1.0)
+
+        def RG1(c, a, eng):
+            st["stg", c] = work.tile([P, 4 * CH], BF16, name="stg", bufs=2, align_bytes=64)
+            regroup(st["stg", c], st["pl", c], eng)
+
+        def RG2(c, a, eng):
+            st["sg", c] = work.tile([P, 4 * CH], BF16, name="sg", bufs=2, align_bytes=64)
+            regroup(st["sg", c], st["sT", c], eng)
+
+        def QS(c, a, eng):
+            st["stq", c] = quantise(st["stg", c], "st_q", 2)
+
+        def QT(c, a, eng):
+            st["sq", c] = quantise(st["sg", c], "s_q", 2)
+
+        def NT(c, u, eng):
+            nzb = psum.tile([P, CH], F32, name="nzb", bufs=2)
+            for s in range(4):
+                nc.tensor.transpose(out=nzb[:, P * s:P * (s + 1)], in_=n_sb[c][:, s, :].bitcast(F32)[:, P * u:P * (u + 1)], identity=ident[:])
+            st["nz", c, u] = nzb
+
+        def DP(c, u, eng):
+            for e in range(2):
+                dp = psum.tile([P, CH], F32, name="dp", bufs=2)
+                mx(dp[:], st["mq", 0], 2 * u + e, st["sq", c])
+                st["dp", c, u, e] = dp
+
+        def SG(c, u, eng):
+            for e in range(2):
+                sgn = psum.tile([P, CH], F32, name="sgn", bufs=2)
+                mx(sgn[:], st["mq", 1], 2 * u + e, st["stq", c])
+                st["sgn", c, u, e] = sgn
+
+        def A(c, u, eng):
+            if u == 0:
+                st["cT", c] = work.tile([P, 4, CH], F32, name="cT", bufs=2)
+            for e in range(2):
+                t = 2 * u + e
+                nc.vector.scalar_tensor_tensor(out=st["cT", c][:, t, :], in0=st["dp", c, u, e][:], scalar=lam_f[:, 0:1],
+                                               in1=st["sT", c][:, t, :], op0=ALU.mult, op1=ALU.mult)
+
+        def B(c, u, eng):
+            nzv = st["nz", c, u][:].bitcast(BF16).rearrange("p (m e) -> p m e", e=2)
+            for e in range(2):
+                t = 2 * u + e
+                nc.vector.scalar_tensor_tensor(out=st["cT", c][:, t, :], in0=nzv[:, :, e], scalar=t01[:, t:t + 1],
+                                               in1=st["cT", c][:, t, :], op0=ALU.mult, op1=ALU.add)
+
+        def C(c, u, eng):
+            for e in range(2):
+                t = 2 * u + e
+                nc.vector.tensor_tensor(out=st["cT", c][:, t, :], in0=st["sgn", c, u, e][:], in1=st["cT", c][:, t, :], op=ALU.add)
+
+        def FP(c, s, eng):
+            if s == 0:
+                st["ob", c] = work.tile([P, 4, D], F32, name="ob", bufs=3)
+            ft = psum.tile([P, 4, P], F32, name="ft", tag="wk", bufs=2)
+            for t in range(4):
+                nc.tensor.transpose(out=ft[:, t, :], in_=st["cT", c][:, t, P * s:P * (s + 1)], identity=ident[:])
+            nc.scalar.activation(out=st["ob", c][:, s, :].rearrange("p (u q e) -> p u q e", u=2, q=P, e=2),
+                                 in_=ft[:].rearrange("p (u e) q -> p u q e", u=2, e=2), func=ACT.Tanh)
+
+        def ST(c, a, eng):
+            nc.sync.dma_start(out=o_v[c], in_=st["ob", c][:])
+
+        tasks = {"WPREP": WPREP, "MK": MK, "QM": QM, "XX": XX, "QX": QX, "PP": PP, "RG1": RG1, "RG2": RG2, "QS": QS, "QT": QT,
+                 "NT": NT, "DP": DP, "SG": SG, "A": A, "B": B, "C": C, "FP": FP, "ST": ST}
+
+        def run(tokens, c):
+            for name, dc, a, eng in tokens:
+                if 0 <= c + dc < NCH:
+                    tasks[name](c + dc, a, eng)
+
+        run(PRO, 0)
+        for c in range(NCH):
+            run(BODY, c)
+        run(EPI, NCH - 1)

@@ -22,8 +22,8 @@ FLOPS = 3 * 2 * M * D * D
 PI_HI = 3.1415927410125732
 PI_LO = math.pi - PI_HI
 
-PRO = [("WPREP", 0, -1, ""), ("XX", 0, 0, "S"), ("XX", 0, 1, "V"), ("QX", 0, -1, ""), ("PP", 0, 2, "V"), ("PP", 0, 0, "S"), ("XX", 1, 0, "S"), ("MK", 0, 0, "V"), ("XX", 1, 1, "V"), ("MK", 0, 1, "G"), ("PP", 0, 1, "V"), ("QX", 1, -1, ""), ("QM", 0, 0, ""), ("QM", 0, 1, ""), ("PP", 0, 3, "S"), ("PP", 1, 0, "S"), ("RG2", 0, -1, "V"), ("PP", 1, 1, "S"), ("QT", 0, -1, ""), ("PP", 1, 2, "S"), ("DP", 0, 0, ""), ("RG1", 0, -1, "G"), ("NT", 0, 0, ""), ("QS", 0, -1, ""), ("PP", 1, 3, "S"), ("SG", 0, 0, "")]
-BODY = [("A", 0, 0, ""), ("DP", 0, 1, ""), ("XX", 2, 0, ""), ("XX", 2, 1, ""), ("B", 0, 0, ""), ("NT", 0, 1, ""), ("NT", 1, 0, ""), ("FP", -1, 0, ""), ("FP", -1, 1, ""), ("FP", -1, 2, ""), ("FP", -1, 3, ""), ("ST", -1, -1, ""), ("C", 0, 0, ""), ("SG", 0, 1, ""), ("A", 0, 1, ""), ("QX", 2, -1, ""), ("PP", 2, 0, ""), ("PP", 2, 1, ""), ("RG2", 1, -1, ""), ("QT", 1, -1, ""), ("DP", 1, 0, ""), ("B", 0, 1, ""), ("PP", 2, 2, ""), ("PP", 2, 3, ""), ("C", 0, 1, ""), ("RG1", 1, -1, ""), ("QS", 1, -1, ""), ("SG", 1, 0, "")]
+PRO = [("WPREP", 0, -1, ""), ("XX", 0, 0, "S"), ("XX", 0, 1, "V"), ("QX", 0, -1, ""), ("PP", 0, 0, "V"), ("PP", 0, 1, "V"), ("PP", 0, 2, "V"), ("XX", 1, 0, "S"), ("MK", 0, 1, "G"), ("XX", 1, 1, "S"), ("MK", 0, 0, "V"), ("QX", 1, -1, ""), ("PP", 0, 3, "S"), ("QM", 0, 0, ""), ("XX", 2, 0, "S"), ("XX", 2, 1, "S"), ("PP", 1, 1, "S"), ("RG1", 0, -1, "V"), ("QM", 0, 1, ""), ("RG2", 0, -1, "V"), ("PP", 1, 2, "S"), ("NT", 0, 0, ""), ("QX", 2, -1, ""), ("PP", 1, 3, "V"), ("PP", 1, 0, "S"), ("QT", 0, -1, ""), ("QS", 0, -1, ""), ("PP", 2, 1, "V"), ("DP", 0, 0, ""), ("XX", 3, 0, "S"), ("RG1", 1, -1, "G"), ("XX", 3, 1, "S"), ("SG", 0, 0, ""), ("RG2", 1, -1, "G"), ("PP", 2, 0, "S")]
+BODY = [("PP", 2, 2, ""), ("A", 0, 0, ""), ("B", 0, 0, ""), ("C", 0, 0, ""), ("DP", 0, 1, ""), ("NT", 0, 1, ""), ("A", 0, 1, ""), ("QX", 3, -1, ""), ("PP", 2, 3, ""), ("QS", 1, -1, ""), ("FP", -1, 0, ""), ("NT", 1, 0, ""), ("FP", -1, 2, ""), ("FP", -1, 3, ""), ("SG", 0, 1, ""), ("XX", 4, 0, ""), ("PP", 3, 0, ""), ("QT", 1, -1, ""), ("B", 0, 1, ""), ("DP", 1, 0, ""), ("FP", -1, 1, ""), ("XX", 4, 1, ""), ("C", 0, 1, ""), ("PP", 3, 1, ""), ("RG1", 2, -1, ""), ("ST", -1, -1, ""), ("RG2", 2, -1, ""), ("SG", 1, 0, "")]
 EPI = [("FP", 0, 0, ""), ("FP", 0, 1, ""), ("FP", 0, 2, ""), ("FP", 0, 3, ""), ("ST", 0, -1, "")]
 
 
@@ -170,7 +170,7 @@ def tile_brainquantumlayer_pa_t_kernel(tc, x, W_in, b_in, weights, J, theta, lam
         def PP(c, t, eng):
             if ("pl", c) not in st:
                 st["pl", c] = work.tile([P, 4, CH], BF16, name="pl", bufs=2)
-                st["sT", c] = work.tile([P, 4, CH], F32, name="sT", bufs=3)
+                st["sT", c] = work.tile([P, 4, CH], F32, name="sT", bufs=4)
             acc = psum.tile([P, CH], F32, name="acc_st", tag="wk", bufs=2)
             mx(acc[:], st["wq"], t, st["xq", c])
             if eng == "V":
@@ -180,11 +180,11 @@ def tile_brainquantumlayer_pa_t_kernel(tc, x, W_in, b_in, weights, J, theta, lam
             nc.scalar.activation(out=st["sT", c][:, t, :], in_=acc[:], func=ACT.Tanh, bias=b_f[:, t:t + 1], scale=1.0)
 
         def RG1(c, a, eng):
-            st["stg", c] = work.tile([P, 4 * CH], BF16, name="stg", bufs=2, align_bytes=64)
+            st["stg", c] = work.tile([P, 4 * CH], BF16, name="stg", bufs=1, align_bytes=64)
             regroup(st["stg", c], st["pl", c], eng)
 
         def RG2(c, a, eng):
-            st["sg", c] = work.tile([P, 4 * CH], BF16, name="sg", bufs=2, align_bytes=64)
+            st["sg", c] = work.tile([P, 4 * CH], BF16, name="sg", bufs=1, align_bytes=64)
             regroup(st["sg", c], st["sT", c], eng)
 
         def QS(c, a, eng):

@@ -14,57 +14,60 @@ ACT = mybir.ActivationFunctionType
 ALU = mybir.AluOpType
 
 P = 128
+PACK = 4
 M, D = 4096, 512
 CH = 512
 NCH = M // CH
+SUB = CH // P
 FLOPS = 3 * 2 * M * D * D
 
 PI_HI = 3.1415927410125732
 PI_LO = math.pi - PI_HI
 
-PRO = [("WPREP", 0, -1, ""), ("XX", 0, 0, "S"), ("XX", 0, 1, "V"), ("QX", 0, -1, ""), ("PP", 0, 0, "V"), ("PP", 0, 1, "V"), ("PP", 0, 2, "V"), ("XX", 1, 0, "S"), ("MK", 0, 1, "G"), ("XX", 1, 1, "S"), ("MK", 0, 0, "V"), ("QX", 1, -1, ""), ("PP", 0, 3, "S"), ("QM", 0, 0, ""), ("XX", 2, 0, "S"), ("XX", 2, 1, "S"), ("PP", 1, 1, "S"), ("RG1", 0, -1, "V"), ("QM", 0, 1, ""), ("RG2", 0, -1, "V"), ("PP", 1, 2, "S"), ("NT", 0, 0, ""), ("QX", 2, -1, ""), ("PP", 1, 3, "V"), ("PP", 1, 0, "S"), ("QT", 0, -1, ""), ("QS", 0, -1, ""), ("PP", 2, 1, "V"), ("DP", 0, 0, ""), ("XX", 3, 0, "S"), ("RG1", 1, -1, "G"), ("XX", 3, 1, "S"), ("SG", 0, 0, ""), ("RG2", 1, -1, "G"), ("PP", 2, 0, "S")]
-BODY = [("PP", 2, 2, ""), ("A", 0, 0, ""), ("B", 0, 0, ""), ("C", 0, 0, ""), ("DP", 0, 1, ""), ("NT", 0, 1, ""), ("A", 0, 1, ""), ("QX", 3, -1, ""), ("PP", 2, 3, ""), ("QS", 1, -1, ""), ("FP", -1, 0, ""), ("NT", 1, 0, ""), ("FP", -1, 2, ""), ("FP", -1, 3, ""), ("SG", 0, 1, ""), ("XX", 4, 0, ""), ("PP", 3, 0, ""), ("QT", 1, -1, ""), ("B", 0, 1, ""), ("DP", 1, 0, ""), ("FP", -1, 1, ""), ("XX", 4, 1, ""), ("C", 0, 1, ""), ("PP", 3, 1, ""), ("RG1", 2, -1, ""), ("ST", -1, -1, ""), ("RG2", 2, -1, ""), ("SG", 1, 0, "")]
-EPI = [("FP", 0, 0, ""), ("FP", 0, 1, ""), ("FP", 0, 2, ""), ("FP", 0, 3, ""), ("ST", 0, -1, "")]
+AHEAD_X = 4
+AHEAD_XQ = 3
+AHEAD_GROUP = 2
+AHEAD_Q = 1
 
 
 def tile_brainquantumlayer_pa_t_kernel(tc, x, W_in, b_in, weights, J, theta, lam, mask, noise_raw, out):
     nc = tc.nc
     with ExitStack() as ctx:
-        ctx.enter_context(tc.manual_schedule())
         keep = ctx.enter_context(tc.tile_pool(name="keep", bufs=1))
         work = ctx.enter_context(tc.tile_pool(name="work", bufs=2))
         psum = ctx.enter_context(tc.psum_pool(name="psum", bufs=2))
 
-        x_v = x.rearrange("(c p s) k -> c p s k", p=P, s=4)
-        n_v = noise_raw.rearrange("(c p s) k -> c p s k", p=P, s=4)
-        o_v = out.rearrange("(c p s) k -> c p s k", p=P, s=4)
+        x_v = x.rearrange("(c p s) k -> c p s k", p=P, s=SUB)
+        n_v = noise_raw.rearrange("(c p s) k -> c p s k", p=P, s=SUB)
+        o_v = out.rearrange("(c p s) k -> c p s k", p=P, s=SUB)
 
-        def load_upe(dst, w):
+        def load_planes(dst, w):
             nc.sync.dma_start(out=dst[:].rearrange("p (u e) j -> p u (e j)", u=2),
                               in_=w.rearrange("(u p e) j -> p u (e j)", u=2, p=P, e=2))
 
-        b_bf = keep.tile([P, 4], BF16, name="b_bf")
-        th_bf = keep.tile([P, 4], BF16, name="th_bf")
+        def load_vector(dst, v):
+            nc.scalar.dma_start(out=dst[:].rearrange("p (u e) -> p u e", u=2),
+                                in_=v.rearrange("(u p e) -> p u e", u=2, p=P, e=2))
+
+        b_bf = keep.tile([P, PACK], BF16, name="b_bf")
+        th_bf = keep.tile([P, PACK], BF16, name="th_bf")
         lam_bf = keep.tile([P, 1], BF16, name="lam_bf")
         with nc.allow_non_contiguous_dma(reason="three small vectors, once"):
-            nc.scalar.dma_start(out=th_bf[:].rearrange("p (u e) -> p u e", u=2), in_=theta.rearrange("(u p e) -> p u e", u=2, p=P, e=2))
-            nc.scalar.dma_start(out=b_bf[:].rearrange("p (u e) -> p u e", u=2), in_=b_in.rearrange("(u p e) -> p u e", u=2, p=P, e=2))
+            load_vector(th_bf, theta)
+            load_vector(b_bf, b_in)
             nc.scalar.dma_start(out=lam_bf[:], in_=lam.partition_broadcast(P))
 
-        w_in_sb = keep.tile([P, 4, D], BF16, name="w_in_sb")
-        load_upe(w_in_sb, W_in)
-        x_sb = []
-        n_sb = []
-        for c in range(NCH):
-            x_sb.append(keep.tile([P, 4, D], BF16, name="x_sb%d" % c))
-            n_sb.append(keep.tile([P, 4, D], BF16, name="n_sb%d" % c))
+        w_in_sb = keep.tile([P, PACK, D], BF16, name="w_in_sb")
+        load_planes(w_in_sb, W_in)
+        x_sb = [keep.tile([P, SUB, D], BF16, name="x_sb%d" % c) for c in range(NCH)]
+        n_sb = [keep.tile([P, SUB, D], BF16, name="n_sb%d" % c) for c in range(NCH)]
         nc.sync.dma_start(out=x_sb[0][:], in_=x_v[0])
-        w_sb = keep.tile([P, 4, D], BF16, name="w_sb")
-        m_sb = keep.tile([P, 4, D], BF16, name="m_sb")
-        j_sb = keep.tile([P, 4, D], BF16, name="j_sb")
-        load_upe(j_sb, J)
-        load_upe(m_sb, mask)
-        load_upe(w_sb, weights)
+        j_sb = keep.tile([P, PACK, D], BF16, name="j_sb")
+        m_sb = keep.tile([P, PACK, D], BF16, name="m_sb")
+        w_sb = keep.tile([P, PACK, D], BF16, name="w_sb")
+        load_planes(j_sb, J)
+        load_planes(m_sb, mask)
+        load_planes(w_sb, weights)
         for c in range(NCH):
             if c + 1 < NCH:
                 nc.sync.dma_start(out=x_sb[c + 1][:], in_=x_v[c + 1])
@@ -73,185 +76,190 @@ def tile_brainquantumlayer_pa_t_kernel(tc, x, W_in, b_in, weights, J, theta, lam
         ident = keep.tile([P, P], F32, name="ident")
         make_identity(nc, ident[:])
 
-        th2 = keep.tile([P, 4], F32, name="th2")
+        th2 = keep.tile([P, PACK], F32, name="th2")
         nc.vector.tensor_scalar_mul(out=th2[:], in0=th_bf[:], scalar1=2.0)
-        kq = keep.tile([P, 4], F32, name="kq")
-        nc.vector.tensor_scalar_mul(out=kq[:], in0=th_bf[:], scalar1=2.0 / math.pi)
-        ki = keep.tile([P, 4], I32, name="ki")
-        nc.vector.tensor_copy(out=ki[:], in_=kq[:])
-        kf = keep.tile([P, 4], F32, name="kf")
-        nc.vector.tensor_copy(out=kf[:], in_=ki[:])
-        y1 = keep.tile([P, 4], F32, name="y1")
-        nc.vector.scalar_tensor_tensor(out=y1[:], in0=kf[:], scalar=-PI_HI, in1=th2[:], op0=ALU.mult, op1=ALU.add)
-        y2 = keep.tile([P, 4], F32, name="y2")
-        nc.vector.scalar_tensor_tensor(out=y2[:], in0=kf[:], scalar=-PI_LO, in1=y1[:], op0=ALU.mult, op1=ALU.add)
-        sn = keep.tile([P, 4], F32, name="sn")
-        nc.scalar.activation(out=sn[:], in_=y2[:], func=ACT.Sin)
-        t01 = keep.tile([P, 4], F32, name="t01")
-        nc.scalar.activation(out=t01[:], in_=sn[:], func=ACT.Abs, scale=0.1)
-        b_f = keep.tile([P, 4], F32, name="b_f")
+        k_f = keep.tile([P, PACK], F32, name="k_f")
+        nc.vector.tensor_scalar_mul(out=k_f[:], in0=th_bf[:], scalar1=2.0 / math.pi)
+        k_i = keep.tile([P, PACK], I32, name="k_i")
+        nc.vector.tensor_copy(out=k_i[:], in_=k_f[:])
+        k_w = keep.tile([P, PACK], F32, name="k_w")
+        nc.vector.tensor_copy(out=k_w[:], in_=k_i[:])
+        y_hi = keep.tile([P, PACK], F32, name="y_hi")
+        nc.vector.scalar_tensor_tensor(out=y_hi[:], in0=k_w[:], scalar=-PI_HI, in1=th2[:], op0=ALU.mult, op1=ALU.add)
+        y = keep.tile([P, PACK], F32, name="y")
+        nc.vector.scalar_tensor_tensor(out=y[:], in0=k_w[:], scalar=-PI_LO, in1=y_hi[:], op0=ALU.mult, op1=ALU.add)
+        sin_y = keep.tile([P, PACK], F32, name="sin_y")
+        nc.scalar.activation(out=sin_y[:], in_=y[:], func=ACT.Sin)
+        gain = keep.tile([P, PACK], F32, name="gain")
+        nc.scalar.activation(out=gain[:], in_=sin_y[:], func=ACT.Abs, scale=0.1)
+        b_f = keep.tile([P, PACK], F32, name="b_f")
         nc.vector.tensor_copy(out=b_f[:], in_=b_bf[:])
         lam_f = keep.tile([P, 1], F32, name="lam_f")
         nc.vector.tensor_copy(out=lam_f[:], in_=lam_bf[:])
 
-        st = {}
+        live = {}
 
-        def grp_tile():
-            return work.tile([P, 4 * D], BF16, name="grp", tag="grp", bufs=3, align_bytes=64)
+        def grouped_tile():
+            return work.tile([P, PACK * D], BF16, name="grouped", tag="grouped", bufs=5, align_bytes=64)
 
-        def t_bank(rows, h):
-            bank = psum.tile([P, 2, 256], F32, name="bank_t", tag="wk", bufs=2)
+        def transpose_words(rows, h):
+            bank = psum.tile([P, 2, 2 * P], F32, name="bank_w", tag="to_scalar", bufs=3)
             for i in range(2):
-                src = rows(2 * h + i).bitcast(F32)
+                words = rows[:, 2 * h + i, :].bitcast(F32)
                 for v in range(2):
-                    nc.tensor.transpose(out=bank[:, v, P * i:P * (i + 1)], in_=src[:, P * v:P * (v + 1)], identity=ident[:])
+                    nc.tensor.transpose(out=bank[:, v, P * i:P * (i + 1)], in_=words[:, P * v:P * (v + 1)], identity=ident[:])
             return bank
 
-        def evac(bank, grouped, h, eng):
-            dst = grouped[:].bitcast(F32).rearrange("p (m v) -> p m v", v=2)[:, 256 * h:256 * (h + 1), :]
+        def leave_bank(bank, grouped, h, on_vector):
+            dst = grouped[:].bitcast(F32).rearrange("p (m v) -> p m v", v=2)[:, 2 * P * h:2 * P * (h + 1), :]
             src = bank[:].rearrange("p v m -> p m v")
-            if eng == "V":
+            if on_vector:
                 nc.vector.tensor_copy(out=dst, in_=src)
             else:
                 nc.scalar.copy(out=dst, in_=src)
 
-        def quantise(grouped, name, bufs):
-            pool = keep if bufs == 1 else work
-            codes = pool.tile([P, D], U32, name=name + "_c", bufs=bufs, align_bytes=64)
-            scales = pool.tile([P, D], U8, name=name + "_s", bufs=bufs, align_bytes=64)
+        def quantise(grouped, name, pool):
+            codes = pool.tile([P, D], U32, name=name + "_c", align_bytes=64)
+            scales = pool.tile([P, D], U8, name=name + "_s", align_bytes=64)
             nc.vector.quantize_mx(out=codes[:].bitcast(FP8X4), scales=scales[:], in_=grouped[:])
             return codes, scales
 
-        def mx(acc, lhs, t, rhs):
+        def mx_pass(acc, stationary, t, moving):
             cols = slice(P * t, P * (t + 1))
-            nc.tensor.matmul_mx(out=acc, lhsT=lhs[0][:, cols].bitcast(FP8X4), lhsT_scale=lhs[1][:, cols],
-                                rhs=rhs[0][:].bitcast(FP8X4), rhs_scale=rhs[1][:], start=True, stop=True)
+            nc.tensor.matmul_mx(out=acc[:], lhsT=stationary[0][:, cols].bitcast(FP8X4), lhsT_scale=stationary[1][:, cols],
+                                rhs=moving[0][:].bitcast(FP8X4), rhs_scale=moving[1][:], start=True, stop=True)
 
-        def regroup(dst, src, eng):
-            if eng == "V":
-                nc.vector.tensor_copy(out=dst[:].rearrange("p (c i t) -> p c t i", i=4, t=4),
-                                      in_=src[:].rearrange("p t (c i) -> p c t i", i=4))
+        def regroup(planes, name, on_vector):
+            grouped = work.tile([P, PACK * CH], BF16, name=name, bufs=1, align_bytes=64)
+            if on_vector:
+                nc.vector.tensor_copy(out=grouped[:].rearrange("p (c i t) -> p c t i", i=4, t=PACK),
+                                      in_=planes[:].rearrange("p t (c i) -> p c t i", i=4))
             else:
-                nc.gpsimd.tensor_scalar(out=dst[:].rearrange("p (m t) -> p m t", t=4), in0=src[:].rearrange("p t m -> p m t"),
+                nc.gpsimd.tensor_scalar(out=grouped[:].rearrange("p (m t) -> p m t", t=PACK), in0=planes[:].rearrange("p t m -> p m t"),
                                         scalar1=1.0, scalar2=0.0, op0=ALU.mult, op1=ALU.add)
+            return grouped
 
-        def WPREP(c, a, eng):
-            wg = grp_tile()
+        def prepare_w_in():
+            grouped = grouped_tile()
             for h in range(2):
-                bank = t_bank(lambda i: w_in_sb[:, i, :], h)
-                evac(bank, wg, h, "V" if h == 0 else "S")
-            st["wq"] = quantise(wg, "w_q", 1)
+                leave_bank(transpose_words(w_in_sb, h), grouped, h, on_vector=(h == 0))
+            live["w_in"] = quantise(grouped, "w_in_q", keep)
 
-        def MK(c, a, eng):
-            g = grp_tile()
-            w = j_sb if a == 0 else w_sb
-            gv = g[:].rearrange("p (u e q t) -> p u e q t", u=2, e=2, q=P, t=4)
-            wv = w[:].rearrange("p t (u q e) -> p u e q t", u=2, q=P, e=2)
-            mv = m_sb[:].rearrange("p t (u q e) -> p u e q t", u=2, q=P, e=2)
+        def mask_weights(w, name):
+            grouped = grouped_tile()
+            g_v = grouped[:].rearrange("p (u e q t) -> p u e q t", u=2, e=2, q=P, t=PACK)
+            w_v = w[:].rearrange("p t (u q e) -> p u e q t", u=2, q=P, e=2)
+            m_v = m_sb[:].rearrange("p t (u q e) -> p u e q t", u=2, q=P, e=2)
             for e in range(2):
-                if eng == "G":
-                    nc.gpsimd.tensor_tensor(out=gv[:, :, e, :, :], in0=wv[:, :, e, :, :], in1=mv[:, :, e, :, :], op=ALU.mult)
-                else:
-                    nc.vector.tensor_tensor(out=gv[:, :, e, :, :], in0=wv[:, :, e, :, :], in1=mv[:, :, e, :, :], op=ALU.mult)
-            st["mg", a] = g
+                nc.vector.tensor_tensor(out=g_v[:, :, e, :, :], in0=w_v[:, :, e, :, :], in1=m_v[:, :, e, :, :], op=ALU.mult)
+            live[name] = grouped
 
-        def QM(c, a, eng):
-            st["mq", a] = quantise(st["mg", a], "m_q%d" % a, 1)
-
-        def XX(c, h, eng):
+        def transpose_x(c, h):
             if h == 0:
-                st["xg", c] = grp_tile()
-            bank = t_bank(lambda i: x_sb[c][:, i, :], h)
-            evac(bank, st["xg", c], h, eng)
+                live["xg", c] = grouped_tile()
+            leave_bank(transpose_words(x_sb[c], h), live["xg", c], h, on_vector=(c == 0 and h == 0))
 
-        def QX(c, a, eng):
-            st["xq", c] = quantise(st["xg", c], "x_q", 2)
+        def quantise_x(c):
+            live["xq", c] = quantise(live["xg", c], "x_q", work)
 
-        def PP(c, t, eng):
-            if ("pl", c) not in st:
-                st["pl", c] = work.tile([P, 4, CH], BF16, name="pl", bufs=2)
-                st["sT", c] = work.tile([P, 4, CH], F32, name="sT", bufs=4)
-            acc = psum.tile([P, CH], F32, name="acc_st", tag="wk", bufs=2)
-            mx(acc[:], st["wq"], t, st["xq", c])
-            if eng == "V":
-                nc.vector.tensor_scalar_add(out=st["pl", c][:, t, :], in0=acc[:], scalar1=b_f[:, t:t + 1])
+        def project(c, t):
+            if t == 0:
+                live["state", c] = work.tile([P, PACK, CH], BF16, name="state_pl", bufs=2)
+                live["s", c] = work.tile([P, PACK, CH], F32, name="s_pl", bufs=4)
+            acc = psum.tile([P, CH], F32, name="acc_state", tag="to_scalar", bufs=3)
+            mx_pass(acc, live["w_in"], t, live["xq", c])
+            if c == 0:
+                nc.vector.tensor_scalar_add(out=live["state", c][:, t, :], in0=acc[:], scalar1=b_f[:, t:t + 1])
             else:
-                nc.scalar.activation(out=st["pl", c][:, t, :], in_=acc[:], func=ACT.Identity, bias=b_f[:, t:t + 1], scale=1.0)
-            nc.scalar.activation(out=st["sT", c][:, t, :], in_=acc[:], func=ACT.Tanh, bias=b_f[:, t:t + 1], scale=1.0)
+                nc.scalar.activation(out=live["state", c][:, t, :], in_=acc[:], func=ACT.Identity, bias=b_f[:, t:t + 1], scale=1.0)
+            nc.scalar.activation(out=live["s", c][:, t, :], in_=acc[:], func=ACT.Tanh, bias=b_f[:, t:t + 1], scale=1.0)
 
-        def RG1(c, a, eng):
-            st["stg", c] = work.tile([P, 4 * CH], BF16, name="stg", bufs=1, align_bytes=64)
-            regroup(st["stg", c], st["pl", c], eng)
+        def regroup_both(c):
+            live["state_g", c] = regroup(live["state", c], "state_g", on_vector=(c == 0))
+            live["s_g", c] = regroup(live["s", c], "s_g", on_vector=(c <= 1))
 
-        def RG2(c, a, eng):
-            st["sg", c] = work.tile([P, 4 * CH], BF16, name="sg", bufs=1, align_bytes=64)
-            regroup(st["sg", c], st["sT", c], eng)
+        def quantise_both(c):
+            live["sq", c] = quantise(live["s_g", c], "s_q", work)
+            live["stq", c] = quantise(live["state_g", c], "state_q", work)
 
-        def QS(c, a, eng):
-            st["stq", c] = quantise(st["stg", c], "st_q", 2)
-
-        def QT(c, a, eng):
-            st["sq", c] = quantise(st["sg", c], "s_q", 2)
-
-        def NT(c, u, eng):
-            nzb = psum.tile([P, CH], F32, name="nzb", bufs=2)
-            for s in range(4):
-                nc.tensor.transpose(out=nzb[:, P * s:P * (s + 1)], in_=n_sb[c][:, s, :].bitcast(F32)[:, P * u:P * (u + 1)], identity=ident[:])
-            st["nz", c, u] = nzb
-
-        def DP(c, u, eng):
+        def recurrent(c, u):
             for e in range(2):
-                dp = psum.tile([P, CH], F32, name="dp", bufs=2)
-                mx(dp[:], st["mq", 0], 2 * u + e, st["sq", c])
-                st["dp", c, u, e] = dp
+                acc = psum.tile([P, CH], F32, name="acc_rec", bufs=2)
+                mx_pass(acc, live["j"], 2 * u + e, live["sq", c])
+                live["rec", c, u, e] = acc
 
-        def SG(c, u, eng):
+        def signal(c, u):
             for e in range(2):
-                sgn = psum.tile([P, CH], F32, name="sgn", bufs=2)
-                mx(sgn[:], st["mq", 1], 2 * u + e, st["stq", c])
-                st["sgn", c, u, e] = sgn
+                acc = psum.tile([P, CH], F32, name="acc_sig", bufs=2)
+                mx_pass(acc, live["w"], 2 * u + e, live["stq", c])
+                live["sig", c, u, e] = acc
 
-        def A(c, u, eng):
+        def transpose_noise(c, u):
+            bank = psum.tile([P, CH], F32, name="bank_n", bufs=1)
+            for s in range(SUB):
+                nc.tensor.transpose(out=bank[:, P * s:P * (s + 1)], in_=n_sb[c][:, s, :].bitcast(F32)[:, P * u:P * (u + 1)], identity=ident[:])
+            live["noise", c, u] = bank
+
+        def add_delta(c, u):
             if u == 0:
-                st["cT", c] = work.tile([P, 4, CH], F32, name="cT", bufs=2)
+                live["sum", c] = work.tile([P, PACK, CH], F32, name="sum_pl", bufs=3)
             for e in range(2):
                 t = 2 * u + e
-                nc.vector.scalar_tensor_tensor(out=st["cT", c][:, t, :], in0=st["dp", c, u, e][:], scalar=lam_f[:, 0:1],
-                                               in1=st["sT", c][:, t, :], op0=ALU.mult, op1=ALU.mult)
+                nc.vector.scalar_tensor_tensor(out=live["sum", c][:, t, :], in0=live["rec", c, u, e][:], scalar=lam_f[:, 0:1],
+                                               in1=live["s", c][:, t, :], op0=ALU.mult, op1=ALU.mult)
 
-        def B(c, u, eng):
-            nzv = st["nz", c, u][:].bitcast(BF16).rearrange("p (m e) -> p m e", e=2)
+        def add_noise(c, u):
+            pairs = live["noise", c, u][:].bitcast(BF16).rearrange("p (m e) -> p m e", e=2)
             for e in range(2):
                 t = 2 * u + e
-                nc.vector.scalar_tensor_tensor(out=st["cT", c][:, t, :], in0=nzv[:, :, e], scalar=t01[:, t:t + 1],
-                                               in1=st["cT", c][:, t, :], op0=ALU.mult, op1=ALU.add)
+                nc.vector.scalar_tensor_tensor(out=live["sum", c][:, t, :], in0=pairs[:, :, e], scalar=gain[:, t:t + 1],
+                                               in1=live["sum", c][:, t, :], op0=ALU.mult, op1=ALU.add)
 
-        def C(c, u, eng):
+        def add_signal(c, u):
             for e in range(2):
                 t = 2 * u + e
-                nc.vector.tensor_tensor(out=st["cT", c][:, t, :], in0=st["sgn", c, u, e][:], in1=st["cT", c][:, t, :], op=ALU.add)
+                nc.vector.tensor_tensor(out=live["sum", c][:, t, :], in0=live["sig", c, u, e][:], in1=live["sum", c][:, t, :], op=ALU.add)
 
-        def FP(c, s, eng):
+        def finish(c, s):
             if s == 0:
-                st["ob", c] = work.tile([P, 4, D], F32, name="ob", bufs=3)
-            ft = psum.tile([P, 4, P], F32, name="ft", tag="wk", bufs=2)
-            for t in range(4):
-                nc.tensor.transpose(out=ft[:, t, :], in_=st["cT", c][:, t, P * s:P * (s + 1)], identity=ident[:])
-            nc.scalar.activation(out=st["ob", c][:, s, :].rearrange("p (u q e) -> p u q e", u=2, q=P, e=2),
-                                 in_=ft[:].rearrange("p (u e) q -> p u q e", u=2, e=2), func=ACT.Tanh)
+                live["out", c] = work.tile([P, SUB, D], F32, name="out_sb", bufs=2)
+            bank = psum.tile([P, PACK, P], F32, name="bank_o", tag="to_scalar", bufs=3)
+            for t in range(PACK):
+                nc.tensor.transpose(out=bank[:, t, :], in_=live["sum", c][:, t, P * s:P * (s + 1)], identity=ident[:])
+            nc.scalar.activation(out=live["out", c][:, s, :].rearrange("p (u q e) -> p u q e", u=2, q=P, e=2),
+                                 in_=bank[:].rearrange("p (u e) q -> p u q e", u=2, e=2), func=ACT.Tanh)
+            if s == SUB - 1:
+                nc.sync.dma_start(out=o_v[c], in_=live["out", c][:])
 
-        def ST(c, a, eng):
-            nc.sync.dma_start(out=o_v[c], in_=st["ob", c][:])
+        def do(stage, c, *args):
+            if 0 <= c < NCH:
+                stage(c, *args)
 
-        tasks = {"WPREP": WPREP, "MK": MK, "QM": QM, "XX": XX, "QX": QX, "PP": PP, "RG1": RG1, "RG2": RG2, "QS": QS, "QT": QT,
-                 "NT": NT, "DP": DP, "SG": SG, "A": A, "B": B, "C": C, "FP": FP, "ST": ST}
+        def half_step(c, u):
+            nxt = (c, 1) if u == 0 else (c + 1, 0)
+            ahead = c + AHEAD_GROUP + u
+            do(add_delta, c, u)
+            do(recurrent, *nxt)
+            do(project, ahead, 2 - 2 * u)
+            do(add_noise, c, u)
+            do(transpose_noise, *nxt)
+            do(finish, c - 1, 2 * u)
+            do(finish, c - 1, 2 * u + 1)
+            do(transpose_x, c + AHEAD_X, u)
+            do(add_signal, c, u)
+            do(signal, *nxt)
+            do(project, ahead, 3 - 2 * u)
 
-        def run(tokens, c):
-            for name, dc, a, eng in tokens:
-                if 0 <= c + dc < NCH:
-                    tasks[name](c + dc, a, eng)
-
-        run(PRO, 0)
-        for c in range(NCH):
-            run(BODY, c)
-        run(EPI, NCH - 1)
+        prepare_w_in()
+        for c in range(-AHEAD_X, NCH + 1):
+            half_step(c, 0)
+            do(quantise_x, c + AHEAD_XQ)
+            if c + AHEAD_XQ == 0:
+                mask_weights(j_sb, "j_g")
+                mask_weights(w_sb, "w_g")
+            if c + AHEAD_XQ == 1:
+                live["j"] = quantise(live["j_g"], "j_q", keep)
+                live["w"] = quantise(live["w_g"], "w_q", keep)
+            do(quantise_both, c + AHEAD_Q)
+            do(regroup_both, c + AHEAD_GROUP)
+            half_step(c, 1)

@@ -42,8 +42,9 @@ def tile_brainquantumlayer_pa_t_kernel(tc, x, W_in, b_in, weights, J, theta, lam
         o_v = out.rearrange("(c p s) k -> c p s k", p=P, s=SUB)
 
         def load_planes(dst, w):
-            nc.sync.dma_start(out=dst[:].rearrange("p (u e) j -> p u (e j)", u=2),
-                              in_=w.rearrange("(u p e) j -> p u (e j)", u=2, p=P, e=2))
+            rows = w.rearrange("(u p e) j -> u p (e j)", u=2, p=P, e=2)
+            for u in range(2):
+                nc.sync.dma_start(out=dst[:, 2 * u:2 * u + 2, :].rearrange("p e j -> p (e j)"), in_=rows[u])
 
         def load_vector(dst, v):
             nc.scalar.dma_start(out=dst[:].rearrange("p (u e) -> p u e", u=2),
@@ -61,7 +62,8 @@ def tile_brainquantumlayer_pa_t_kernel(tc, x, W_in, b_in, weights, J, theta, lam
         load_planes(w_in_sb, W_in)
         x_sb = [keep.tile([P, SUB, D], BF16, name="x_sb%d" % c) for c in range(NCH)]
         n_sb = [keep.tile([P, SUB, D], BF16, name="n_sb%d" % c) for c in range(NCH)]
-        nc.sync.dma_start(out=x_sb[0][:], in_=x_v[0])
+        for h in range(2):
+            nc.sync.dma_start(out=x_sb[0][:, 2 * h:2 * h + 2, :], in_=x_v[0][:, 2 * h:2 * h + 2, :])
         j_sb = keep.tile([P, PACK, D], BF16, name="j_sb")
         m_sb = keep.tile([P, PACK, D], BF16, name="m_sb")
         w_sb = keep.tile([P, PACK, D], BF16, name="w_sb")
@@ -100,7 +102,7 @@ def tile_brainquantumlayer_pa_t_kernel(tc, x, W_in, b_in, weights, J, theta, lam
         live = {}
 
         def grouped_tile():
-            return work.tile([P, PACK * D], BF16, name="grouped", tag="grouped", bufs=5, align_bytes=64)
+            return work.tile([P, PACK * D], BF16, name="grouped", tag="grouped", bufs=4, align_bytes=64)
 
         def transpose_words(rows, h):
             bank = psum.tile([P, 2, 2 * P], F32, name="bank_w", tag="to_scalar", bufs=3)
@@ -215,21 +217,33 @@ def tile_brainquantumlayer_pa_t_kernel(tc, x, W_in, b_in, weights, J, theta, lam
                 nc.vector.scalar_tensor_tensor(out=live["sum", c][:, t, :], in0=pairs[:, :, e], scalar=gain[:, t:t + 1],
                                                in1=live["sum", c][:, t, :], op0=ALU.mult, op1=ALU.add)
 
+        def scalar_helps(c):
+            return c % 2 == 0
+
         def add_signal(c, u):
+            if scalar_helps(c) and u == 0:
+                live["sig_pl", c] = work.tile([P, PACK, CH], F32, name="sig_pl", bufs=2)
             for e in range(2):
                 t = 2 * u + e
-                nc.vector.tensor_tensor(out=live["sum", c][:, t, :], in0=live["sig", c, u, e][:], in1=live["sum", c][:, t, :], op=ALU.add)
+                if scalar_helps(c):
+                    nc.scalar.copy(out=live["sig_pl", c][:, t, :], in_=live["sig", c, u, e][:])
+                else:
+                    nc.vector.tensor_tensor(out=live["sum", c][:, t, :], in0=live["sig", c, u, e][:], in1=live["sum", c][:, t, :], op=ALU.add)
 
         def finish(c, s):
             if s == 0:
                 live["out", c] = work.tile([P, SUB, D], F32, name="out_sb", bufs=2)
             bank = psum.tile([P, PACK, P], F32, name="bank_o", tag="to_scalar", bufs=3)
+            rows = slice(P * s, P * (s + 1))
             for t in range(PACK):
-                nc.tensor.transpose(out=bank[:, t, :], in_=live["sum", c][:, t, P * s:P * (s + 1)], identity=ident[:])
+                if scalar_helps(c):
+                    nc.tensor.matmul(out=bank[:, t, :], lhsT=live["sum", c][:, t, rows], rhs=ident[:], is_transpose=True, start=True, stop=False)
+                    nc.tensor.matmul(out=bank[:, t, :], lhsT=live["sig_pl", c][:, t, rows], rhs=ident[:], is_transpose=True, start=False, stop=True)
+                else:
+                    nc.tensor.transpose(out=bank[:, t, :], in_=live["sum", c][:, t, rows], identity=ident[:])
             nc.scalar.activation(out=live["out", c][:, s, :].rearrange("p (u q e) -> p u q e", u=2, q=P, e=2),
                                  in_=bank[:].rearrange("p (u e) q -> p u q e", u=2, e=2), func=ACT.Tanh)
-            if s == SUB - 1:
-                nc.sync.dma_start(out=o_v[c], in_=live["out", c][:])
+            nc.sync.dma_start(out=o_v[c][:, s, :], in_=live["out", c][:, s, :])
 
         def do(stage, c, *args):
             if 0 <= c < NCH:

@@ -28,6 +28,7 @@ AHEAD_X = 4
 AHEAD_XQ = 3
 AHEAD_GROUP = 2
 AHEAD_Q = 1
+HURRIED = 2
 
 
 def tile_brainquantumlayer_pa_t_kernel(tc, x, W_in, b_in, weights, J, theta, lam, mask, noise_raw, out):
@@ -102,7 +103,7 @@ def tile_brainquantumlayer_pa_t_kernel(tc, x, W_in, b_in, weights, J, theta, lam
         live = {}
 
         def grouped_tile():
-            return work.tile([P, PACK * D], BF16, name="grouped", tag="grouped", bufs=4, align_bytes=64)
+            return work.tile([P, PACK * D], BF16, name="grouped", tag="grouped", bufs=5, align_bytes=64)
 
         def transpose_words(rows, h):
             bank = psum.tile([P, 2, 2 * P], F32, name="bank_w", tag="to_scalar", bufs=3)
@@ -159,7 +160,7 @@ def tile_brainquantumlayer_pa_t_kernel(tc, x, W_in, b_in, weights, J, theta, lam
         def transpose_x(c, h):
             if h == 0:
                 live["xg", c] = grouped_tile()
-            leave_bank(transpose_words(x_sb[c], h), live["xg", c], h, on_vector=(c == 0 and h == 0))
+            leave_bank(transpose_words(x_sb[c], h), live["xg", c], h, on_vector=(c == 0))
 
         def quantise_x(c):
             live["xq", c] = quantise(live["xg", c], "x_q", work)
@@ -170,15 +171,12 @@ def tile_brainquantumlayer_pa_t_kernel(tc, x, W_in, b_in, weights, J, theta, lam
                 live["s", c] = work.tile([P, PACK, CH], F32, name="s_pl", bufs=4)
             acc = psum.tile([P, CH], F32, name="acc_state", tag="to_scalar", bufs=3)
             mx_pass(acc, live["w_in"], t, live["xq", c])
-            if c == 0:
-                nc.vector.tensor_scalar_add(out=live["state", c][:, t, :], in0=acc[:], scalar1=b_f[:, t:t + 1])
-            else:
-                nc.scalar.activation(out=live["state", c][:, t, :], in_=acc[:], func=ACT.Identity, bias=b_f[:, t:t + 1], scale=1.0)
+            nc.scalar.activation(out=live["state", c][:, t, :], in_=acc[:], func=ACT.Identity, bias=b_f[:, t:t + 1], scale=1.0)
             nc.scalar.activation(out=live["s", c][:, t, :], in_=acc[:], func=ACT.Tanh, bias=b_f[:, t:t + 1], scale=1.0)
 
         def regroup_both(c):
-            live["state_g", c] = regroup(live["state", c], "state_g", on_vector=(c == 0))
-            live["s_g", c] = regroup(live["s", c], "s_g", on_vector=(c <= 1))
+            live["s_g", c] = regroup(live["s", c], "s_g", on_vector=(c < HURRIED))
+            live["state_g", c] = regroup(live["state", c], "state_g", on_vector=(c < HURRIED))
 
         def quantise_both(c):
             live["sq", c] = quantise(live["s_g", c], "s_q", work)
@@ -217,33 +215,23 @@ def tile_brainquantumlayer_pa_t_kernel(tc, x, W_in, b_in, weights, J, theta, lam
                 nc.vector.scalar_tensor_tensor(out=live["sum", c][:, t, :], in0=pairs[:, :, e], scalar=gain[:, t:t + 1],
                                                in1=live["sum", c][:, t, :], op0=ALU.mult, op1=ALU.add)
 
-        def scalar_helps(c):
-            return c % 2 == 0
-
         def add_signal(c, u):
-            if scalar_helps(c) and u == 0:
-                live["sig_pl", c] = work.tile([P, PACK, CH], F32, name="sig_pl", bufs=2)
             for e in range(2):
                 t = 2 * u + e
-                if scalar_helps(c):
-                    nc.scalar.copy(out=live["sig_pl", c][:, t, :], in_=live["sig", c, u, e][:])
-                else:
-                    nc.vector.tensor_tensor(out=live["sum", c][:, t, :], in0=live["sig", c, u, e][:], in1=live["sum", c][:, t, :], op=ALU.add)
+                nc.vector.tensor_tensor(out=live["sum", c][:, t, :], in0=live["sig", c, u, e][:], in1=live["sum", c][:, t, :], op=ALU.add)
 
         def finish(c, s):
             if s == 0:
                 live["out", c] = work.tile([P, SUB, D], F32, name="out_sb", bufs=2)
             bank = psum.tile([P, PACK, P], F32, name="bank_o", tag="to_scalar", bufs=3)
-            rows = slice(P * s, P * (s + 1))
             for t in range(PACK):
-                if scalar_helps(c):
-                    nc.tensor.matmul(out=bank[:, t, :], lhsT=live["sum", c][:, t, rows], rhs=ident[:], is_transpose=True, start=True, stop=False)
-                    nc.tensor.matmul(out=bank[:, t, :], lhsT=live["sig_pl", c][:, t, rows], rhs=ident[:], is_transpose=True, start=False, stop=True)
-                else:
-                    nc.tensor.transpose(out=bank[:, t, :], in_=live["sum", c][:, t, rows], identity=ident[:])
+                nc.tensor.transpose(out=bank[:, t, :], in_=live["sum", c][:, t, P * s:P * (s + 1)], identity=ident[:])
             nc.scalar.activation(out=live["out", c][:, s, :].rearrange("p (u q e) -> p u q e", u=2, q=P, e=2),
                                  in_=bank[:].rearrange("p (u e) q -> p u q e", u=2, e=2), func=ACT.Tanh)
-            nc.sync.dma_start(out=o_v[c][:, s, :], in_=live["out", c][:, s, :])
+            if c == NCH - 1:
+                nc.sync.dma_start(out=o_v[c][:, s, :], in_=live["out", c][:, s, :])
+            elif s == SUB - 1:
+                nc.sync.dma_start(out=o_v[c], in_=live["out", c][:])
 
         def do(stage, c, *args):
             if 0 <= c < NCH:

@@ -23,12 +23,10 @@ FLOPS = 3 * 2 * M * D * D
 
 PI_HI = 3.1415927410125732
 PI_LO = math.pi - PI_HI
+SIN_SERIES = [(-1.0) ** i / math.factorial(2 * i + 1) for i in range(11)]
 
-AHEAD_X = 4
-AHEAD_XQ = 3
-AHEAD_GROUP = 2
-AHEAD_Q = 1
-HURRIED = 2
+HURRIED = 1
+CATCH_UP = 3
 
 
 def tile_brainquantumlayer_pa_t_kernel(tc, x, W_in, b_in, weights, J, theta, lam, mask, noise_raw, out):
@@ -76,6 +74,11 @@ def tile_brainquantumlayer_pa_t_kernel(tc, x, W_in, b_in, weights, J, theta, lam
                 nc.sync.dma_start(out=x_sb[c + 1][:], in_=x_v[c + 1])
             nc.sync.dma_start(out=n_sb[c][:], in_=n_v[c])
 
+        first = keep.tile([P, 1], F32, name="first")
+        nc.vector.memset(first[:], 0.0)
+        first_tanh = keep.tile([P, 1], F32, name="first_tanh")
+        nc.scalar.activation(out=first_tanh[:], in_=first[:], func=ACT.Tanh)
+
         ident = keep.tile([P, P], F32, name="ident")
         make_identity(nc, ident[:])
 
@@ -91,15 +94,25 @@ def tile_brainquantumlayer_pa_t_kernel(tc, x, W_in, b_in, weights, J, theta, lam
         nc.vector.scalar_tensor_tensor(out=y_hi[:], in0=k_w[:], scalar=-PI_HI, in1=th2[:], op0=ALU.mult, op1=ALU.add)
         y = keep.tile([P, PACK], F32, name="y")
         nc.vector.scalar_tensor_tensor(out=y[:], in0=k_w[:], scalar=-PI_LO, in1=y_hi[:], op0=ALU.mult, op1=ALU.add)
-        sin_y = keep.tile([P, PACK], F32, name="sin_y")
-        nc.scalar.activation(out=sin_y[:], in_=y[:], func=ACT.Sin)
+        y_01 = keep.tile([P, PACK], F32, name="y_01")
+        nc.vector.tensor_scalar_mul(out=y_01[:], in0=y[:], scalar1=0.1)
+        z = keep.tile([P, PACK], F32, name="z")
+        nc.gpsimd.tensor_tensor(out=z[:], in0=y[:], in1=y[:], op=ALU.mult)
+        q = keep.tile([P, PACK], F32, name="q_top")
+        nc.gpsimd.tensor_scalar(out=q[:], in0=z[:], scalar1=SIN_SERIES[-1], scalar2=0.0, op0=ALU.mult, op1=ALU.add)
+        for i in range(len(SIN_SERIES) - 2, -1, -1):
+            q_c = keep.tile([P, PACK], F32, name="q_c%d" % i)
+            nc.gpsimd.tensor_scalar(out=q_c[:], in0=q[:], scalar1=1.0, scalar2=SIN_SERIES[i], op0=ALU.mult, op1=ALU.add)
+            q = keep.tile([P, PACK], F32, name="q%d" % i)
+            nc.gpsimd.tensor_tensor(out=q[:], in0=q_c[:], in1=z[:] if i else y_01[:], op=ALU.mult)
+        sin_y = q
         gain = keep.tile([P, PACK], F32, name="gain")
-        nc.scalar.activation(out=gain[:], in_=sin_y[:], func=ACT.Abs, scale=0.1)
         b_f = keep.tile([P, PACK], F32, name="b_f")
         nc.vector.tensor_copy(out=b_f[:], in_=b_bf[:])
         lam_f = keep.tile([P, 1], F32, name="lam_f")
         nc.vector.tensor_copy(out=lam_f[:], in_=lam_bf[:])
 
+        done = set()
         live = {}
 
         def grouped_tile():
@@ -146,7 +159,10 @@ def tile_brainquantumlayer_pa_t_kernel(tc, x, W_in, b_in, weights, J, theta, lam
             grouped = grouped_tile()
             for h in range(2):
                 leave_bank(transpose_words(w_in_sb, h), grouped, h, on_vector=(h == 0))
-            live["w_in"] = quantise(grouped, "w_in_q", keep)
+            live["w_in_g"] = grouped
+
+        def quantise_w_in():
+            live["w_in"] = quantise(live["w_in_g"], "w_in_q", keep)
 
         def mask_weights(w, name):
             grouped = grouped_tile()
@@ -160,7 +176,7 @@ def tile_brainquantumlayer_pa_t_kernel(tc, x, W_in, b_in, weights, J, theta, lam
         def transpose_x(c, h):
             if h == 0:
                 live["xg", c] = grouped_tile()
-            leave_bank(transpose_words(x_sb[c], h), live["xg", c], h, on_vector=(c == 0))
+            leave_bank(transpose_words(x_sb[c], h), live["xg", c], h, on_vector=(c == 0 and h == 0))
 
         def quantise_x(c):
             live["xq", c] = quantise(live["xg", c], "x_q", work)
@@ -171,26 +187,48 @@ def tile_brainquantumlayer_pa_t_kernel(tc, x, W_in, b_in, weights, J, theta, lam
                 live["s", c] = work.tile([P, PACK, CH], F32, name="s_pl", bufs=4)
             acc = psum.tile([P, CH], F32, name="acc_state", tag="to_scalar", bufs=3)
             mx_pass(acc, live["w_in"], t, live["xq", c])
-            nc.scalar.activation(out=live["state", c][:, t, :], in_=acc[:], func=ACT.Identity, bias=b_f[:, t:t + 1], scale=1.0)
+            leave_s(c, t, acc)
+            leave_state(c, t, acc)
+
+        def leave_s(c, t, acc):
             nc.scalar.activation(out=live["s", c][:, t, :], in_=acc[:], func=ACT.Tanh, bias=b_f[:, t:t + 1], scale=1.0)
 
-        def regroup_both(c):
+        def leave_state(c, t, acc):
+            nc.scalar.activation(out=live["state", c][:, t, :], in_=acc[:], func=ACT.Identity, bias=b_f[:, t:t + 1], scale=1.0)
+
+        def project_first():
+            live["state", 0] = work.tile([P, PACK, CH], BF16, name="state_pl", bufs=2)
+            live["s", 0] = work.tile([P, PACK, CH], F32, name="s_pl", bufs=4)
+            accs = []
+            for t in range(PACK):
+                acc = psum.tile([P, CH], F32, name="acc_first", tag="acc_rec" if t < 2 else "acc_sig", bufs=2)
+                mx_pass(acc, live["w_in"], t, live["xq", 0])
+                accs.append(acc)
+            for t in range(PACK):
+                done.add((project, 0, (t,)))
+            return accs
+
+        def regroup_s(c):
             live["s_g", c] = regroup(live["s", c], "s_g", on_vector=(c < HURRIED))
+
+        def regroup_state(c):
             live["state_g", c] = regroup(live["state", c], "state_g", on_vector=(c < HURRIED))
 
-        def quantise_both(c):
+        def quantise_s(c):
             live["sq", c] = quantise(live["s_g", c], "s_q", work)
+
+        def quantise_state(c):
             live["stq", c] = quantise(live["state_g", c], "state_q", work)
 
         def recurrent(c, u):
             for e in range(2):
-                acc = psum.tile([P, CH], F32, name="acc_rec", bufs=2)
+                acc = psum.tile([P, CH], F32, name="acc_rec", tag="acc_rec", bufs=2)
                 mx_pass(acc, live["j"], 2 * u + e, live["sq", c])
                 live["rec", c, u, e] = acc
 
         def signal(c, u):
             for e in range(2):
-                acc = psum.tile([P, CH], F32, name="acc_sig", bufs=2)
+                acc = psum.tile([P, CH], F32, name="acc_sig", tag="acc_sig", bufs=2)
                 mx_pass(acc, live["w"], 2 * u + e, live["stq", c])
                 live["sig", c, u, e] = acc
 
@@ -234,34 +272,84 @@ def tile_brainquantumlayer_pa_t_kernel(tc, x, W_in, b_in, weights, J, theta, lam
                 nc.sync.dma_start(out=o_v[c], in_=live["out", c][:])
 
         def do(stage, c, *args):
-            if 0 <= c < NCH:
+            if 0 <= c < NCH and (stage, c, args) not in done:
+                done.add((stage, c, args))
                 stage(c, *args)
 
+        def project_up_to(n):
+            for i in range(min(n, PACK * NCH)):
+                do(project, i // PACK, i % PACK)
+
+        def transpose_both(c):
+            do(transpose_x, c, 0)
+            do(transpose_x, c, 1)
+
+        def quantise_both(c):
+            do(quantise_s, c)
+            do(quantise_state, c)
+
+        def regroup_both(n):
+            do(regroup_s, n // PACK - 1)
+            do(regroup_state, n // PACK - 1)
+
         def half_step(c, u):
+            h = 2 * c + u
             nxt = (c, 1) if u == 0 else (c + 1, 0)
-            ahead = c + AHEAD_GROUP + u
+            planes = min(2 * h + 12, max(3 * h + 7, 8))
+            late = u == 1 and c < CATCH_UP
             do(add_delta, c, u)
-            do(recurrent, *nxt)
-            do(project, ahead, 2 - 2 * u)
+            if not late:
+                do(recurrent, *nxt)
+            project_up_to(planes - 1)
             do(add_noise, c, u)
             do(transpose_noise, *nxt)
+            if late:
+                quantise_both(c + 1)
+                do(recurrent, *nxt)
             do(finish, c - 1, 2 * u)
             do(finish, c - 1, 2 * u + 1)
-            do(transpose_x, c + AHEAD_X, u)
+            if h < 4:
+                transpose_both(h + 2)
+            else:
+                do(transpose_x, c + 4, u)
             do(add_signal, c, u)
             do(signal, *nxt)
-            do(project, ahead, 3 - 2 * u)
+            project_up_to(planes)
+            if u == 0:
+                do(quantise_x, c + 3 if c else 2)
+                if c >= CATCH_UP:
+                    quantise_both(c + 1)
+            elif c == 0:
+                do(quantise_x, 3)
+            regroup_both(planes)
 
-        prepare_w_in()
-        for c in range(-AHEAD_X, NCH + 1):
+        with tc.manual_schedule(engines={mybir.EngineType.PE, mybir.EngineType.Activation, mybir.EngineType.DVE}):
+            prepare_w_in()
+            transpose_both(0)
+            quantise_w_in()
+            do(quantise_x, 0)
+            accs = project_first()
+            mask_weights(j_sb, "j_g")
+            live["j"] = quantise(live["j_g"], "j_q", keep)
+            for t in range(PACK):
+                leave_s(0, t, accs[t])
+            leave_state(0, 0, accs[0])
+            transpose_both(1)
+            for t in range(1, PACK):
+                leave_state(0, t, accs[t])
+            do(regroup_s, 0)
+            do(quantise_s, 0)
+            do(recurrent, 0, 0)
+            do(transpose_noise, 0, 0)
+            do(quantise_x, 1)
+            project_up_to(2 * PACK)
+            mask_weights(w_sb, "w_g")
+            live["w"] = quantise(live["w_g"], "w_q", keep)
+            do(regroup_state, 0)
+            do(quantise_state, 0)
+            do(signal, 0, 0)
+            nc.vector.scalar_tensor_tensor(out=gain[:], in0=sin_y[:], scalar=-1.0, in1=sin_y[:], op0=ALU.mult, op1=ALU.max)
+
+        for c in range(NCH + 1):
             half_step(c, 0)
-            do(quantise_x, c + AHEAD_XQ)
-            if c + AHEAD_XQ == 0:
-                mask_weights(j_sb, "j_g")
-                mask_weights(w_sb, "w_g")
-            if c + AHEAD_XQ == 1:
-                live["j"] = quantise(live["j_g"], "j_q", keep)
-                live["w"] = quantise(live["w_g"], "w_q", keep)
-            do(quantise_both, c + AHEAD_Q)
-            do(regroup_both, c + AHEAD_GROUP)
             half_step(c, 1)

@@ -23,10 +23,7 @@ FLOPS = 3 * 2 * M * D * D
 
 PI_HI = 3.1415927410125732
 PI_LO = math.pi - PI_HI
-SIN_SERIES = [(-1.0) ** i / math.factorial(2 * i + 1) for i in range(11)]
-
-HURRIED = 1
-CATCH_UP = 3
+HURRIED = 2
 
 
 def tile_brainquantumlayer_pa_t_kernel(tc, x, W_in, b_in, weights, J, theta, lam, mask, noise_raw, out):
@@ -74,11 +71,6 @@ def tile_brainquantumlayer_pa_t_kernel(tc, x, W_in, b_in, weights, J, theta, lam
                 nc.sync.dma_start(out=x_sb[c + 1][:], in_=x_v[c + 1])
             nc.sync.dma_start(out=n_sb[c][:], in_=n_v[c])
 
-        first = keep.tile([P, 1], F32, name="first")
-        nc.vector.memset(first[:], 0.0)
-        first_tanh = keep.tile([P, 1], F32, name="first_tanh")
-        nc.scalar.activation(out=first_tanh[:], in_=first[:], func=ACT.Tanh)
-
         ident = keep.tile([P, P], F32, name="ident")
         make_identity(nc, ident[:])
 
@@ -94,19 +86,12 @@ def tile_brainquantumlayer_pa_t_kernel(tc, x, W_in, b_in, weights, J, theta, lam
         nc.vector.scalar_tensor_tensor(out=y_hi[:], in0=k_w[:], scalar=-PI_HI, in1=th2[:], op0=ALU.mult, op1=ALU.add)
         y = keep.tile([P, PACK], F32, name="y")
         nc.vector.scalar_tensor_tensor(out=y[:], in0=k_w[:], scalar=-PI_LO, in1=y_hi[:], op0=ALU.mult, op1=ALU.add)
-        y_01 = keep.tile([P, PACK], F32, name="y_01")
-        nc.vector.tensor_scalar_mul(out=y_01[:], in0=y[:], scalar1=0.1)
-        z = keep.tile([P, PACK], F32, name="z")
-        nc.gpsimd.tensor_tensor(out=z[:], in0=y[:], in1=y[:], op=ALU.mult)
-        q = keep.tile([P, PACK], F32, name="q_top")
-        nc.gpsimd.tensor_scalar(out=q[:], in0=z[:], scalar1=SIN_SERIES[-1], scalar2=0.0, op0=ALU.mult, op1=ALU.add)
-        for i in range(len(SIN_SERIES) - 2, -1, -1):
-            q_c = keep.tile([P, PACK], F32, name="q_c%d" % i)
-            nc.gpsimd.tensor_scalar(out=q_c[:], in0=q[:], scalar1=1.0, scalar2=SIN_SERIES[i], op0=ALU.mult, op1=ALU.add)
-            q = keep.tile([P, PACK], F32, name="q%d" % i)
-            nc.gpsimd.tensor_tensor(out=q[:], in0=q_c[:], in1=z[:] if i else y_01[:], op=ALU.mult)
-        sin_y = q
+        sin_y = keep.tile([P, PACK], F32, name="sin_y")
+        nc.scalar.activation(out=sin_y[:], in_=y[:], func=ACT.Sin)
+        first_tanh = keep.tile([P, PACK], F32, name="first_tanh")
+        nc.scalar.activation(out=first_tanh[:], in_=sin_y[:], func=ACT.Tanh)
         gain = keep.tile([P, PACK], F32, name="gain")
+        nc.scalar.activation(out=gain[:], in_=sin_y[:], func=ACT.Abs, scale=0.1)
         b_f = keep.tile([P, PACK], F32, name="b_f")
         nc.vector.tensor_copy(out=b_f[:], in_=b_bf[:])
         lam_f = keep.tile([P, 1], F32, name="lam_f")
@@ -158,7 +143,7 @@ def tile_brainquantumlayer_pa_t_kernel(tc, x, W_in, b_in, weights, J, theta, lam
         def prepare_w_in():
             grouped = grouped_tile()
             for h in range(2):
-                leave_bank(transpose_words(w_in_sb, h), grouped, h, on_vector=(h == 0))
+                leave_bank(transpose_words(w_in_sb, h), grouped, h, on_vector=True)
             live["w_in_g"] = grouped
 
         def quantise_w_in():
@@ -295,32 +280,21 @@ def tile_brainquantumlayer_pa_t_kernel(tc, x, W_in, b_in, weights, J, theta, lam
         def half_step(c, u):
             h = 2 * c + u
             nxt = (c, 1) if u == 0 else (c + 1, 0)
-            planes = min(2 * h + 12, max(3 * h + 7, 8))
-            late = u == 1 and c < CATCH_UP
+            planes = 2 * h + 12 if h > 1 else 3 * h + 10
             do(add_delta, c, u)
-            if not late:
-                do(recurrent, *nxt)
+            do(recurrent, *nxt)
             project_up_to(planes - 1)
             do(add_noise, c, u)
             do(transpose_noise, *nxt)
-            if late:
-                quantise_both(c + 1)
-                do(recurrent, *nxt)
             do(finish, c - 1, 2 * u)
             do(finish, c - 1, 2 * u + 1)
-            if h < 4:
-                transpose_both(h + 2)
-            else:
-                do(transpose_x, c + 4, u)
+            do(transpose_x, c + 4, u)
             do(add_signal, c, u)
             do(signal, *nxt)
             project_up_to(planes)
-            if u == 0:
-                do(quantise_x, c + 3 if c else 2)
-                if c >= CATCH_UP:
-                    quantise_both(c + 1)
-            elif c == 0:
-                do(quantise_x, 3)
+            if u == 0 and c > 0:
+                do(quantise_x, c + 3)
+                quantise_both(c + 1)
             regroup_both(planes)
 
         with tc.manual_schedule(engines={mybir.EngineType.PE, mybir.EngineType.Activation, mybir.EngineType.DVE}):
@@ -348,7 +322,18 @@ def tile_brainquantumlayer_pa_t_kernel(tc, x, W_in, b_in, weights, J, theta, lam
             do(regroup_state, 0)
             do(quantise_state, 0)
             do(signal, 0, 0)
-            nc.vector.scalar_tensor_tensor(out=gain[:], in0=sin_y[:], scalar=-1.0, in1=sin_y[:], op0=ALU.mult, op1=ALU.max)
+            do(add_delta, 0, 0)
+            do(recurrent, 0, 1)
+            do(add_noise, 0, 0)
+            do(transpose_noise, 0, 1)
+            transpose_both(2)
+            transpose_both(3)
+            do(regroup_s, 1)
+            do(quantise_s, 1)
+            do(quantise_x, 2)
+            do(regroup_state, 1)
+            do(quantise_state, 1)
+            do(quantise_x, 3)
 
         for c in range(NCH + 1):
             half_step(c, 0)

@@ -280,7 +280,7 @@ def tile_brainquantumlayer_pa_t_kernel(tc, x, W_in, b_in, weights, J, theta, lam
         def half_step(c, u):
             h = 2 * c + u
             nxt = (c, 1) if u == 0 else (c + 1, 0)
-            planes = 2 * h + 12 if h > 1 else 3 * h + 10
+            planes = 2 * h + 12
             do(add_delta, c, u)
             do(recurrent, *nxt)
             project_up_to(planes - 1)
@@ -311,12 +311,14 @@ def tile_brainquantumlayer_pa_t_kernel(tc, x, W_in, b_in, weights, J, theta, lam
             transpose_both(1)
             for t in range(1, PACK):
                 leave_state(0, t, accs[t])
+            transpose_both(2)
             do(regroup_s, 0)
             do(quantise_s, 0)
             do(recurrent, 0, 0)
             do(transpose_noise, 0, 0)
             do(quantise_x, 1)
-            project_up_to(2 * PACK)
+            do(quantise_x, 2)
+            project_up_to(2 * PACK + 2)
             mask_weights(w_sb, "w_g")
             live["w"] = quantise(live["w_g"], "w_q", keep)
             do(regroup_state, 0)
@@ -326,11 +328,10 @@ def tile_brainquantumlayer_pa_t_kernel(tc, x, W_in, b_in, weights, J, theta, lam
             do(recurrent, 0, 1)
             do(add_noise, 0, 0)
             do(transpose_noise, 0, 1)
-            transpose_both(2)
             transpose_both(3)
+            project_up_to(3 * PACK)
             do(regroup_s, 1)
             do(quantise_s, 1)
-            do(quantise_x, 2)
             do(regroup_state, 1)
             do(quantise_state, 1)
             do(quantise_x, 3)

@@ -24,6 +24,7 @@ FLOPS = 3 * 2 * M * D * D
 PI_HI = 3.1415927410125732
 PI_LO = math.pi - PI_HI
 HURRIED = 2
+MIXED = (NCH - 2, NCH - 1)
 
 
 def tile_brainquantumlayer_pa_t_kernel(tc, x, W_in, b_in, weights, J, theta, lam, mask, noise_raw, out):
@@ -221,7 +222,11 @@ def tile_brainquantumlayer_pa_t_kernel(tc, x, W_in, b_in, weights, J, theta, lam
             bank = psum.tile([P, CH], F32, name="bank_n", bufs=1)
             for s in range(SUB):
                 nc.tensor.transpose(out=bank[:, P * s:P * (s + 1)], in_=n_sb[c][:, s, :].bitcast(F32)[:, P * u:P * (u + 1)], identity=ident[:])
-            live["noise", c, u] = bank
+            if c in MIXED:
+                words = work.tile([P, CH], F32, name="noise_sb", bufs=3)
+                nc.scalar.copy(out=words[:], in_=bank[:])
+                bank = words
+            live["noise", c, u] = bank[:].bitcast(BF16).rearrange("p (m e) -> p m e", e=2)
 
         def add_delta(c, u):
             if u == 0:
@@ -232,13 +237,22 @@ def tile_brainquantumlayer_pa_t_kernel(tc, x, W_in, b_in, weights, J, theta, lam
                                                in1=live["s", c][:, t, :], op0=ALU.mult, op1=ALU.mult)
 
         def add_noise(c, u):
-            pairs = live["noise", c, u][:].bitcast(BF16).rearrange("p (m e) -> p m e", e=2)
+            if c in MIXED:
+                return
             for e in range(2):
                 t = 2 * u + e
-                nc.vector.scalar_tensor_tensor(out=live["sum", c][:, t, :], in0=pairs[:, :, e], scalar=gain[:, t:t + 1],
+                nc.vector.scalar_tensor_tensor(out=live["sum", c][:, t, :], in0=live["noise", c, u][:, :, e], scalar=gain[:, t:t + 1],
                                                in1=live["sum", c][:, t, :], op0=ALU.mult, op1=ALU.add)
 
         def add_signal(c, u):
+            if c in MIXED:
+                if u == 0:
+                    live["sum2", c] = work.tile([P, PACK, CH], F32, name="sum2_pl", bufs=2)
+                for e in range(2):
+                    t = 2 * u + e
+                    nc.vector.scalar_tensor_tensor(out=live["sum2", c][:, t, :], in0=live["noise", c, u][:, :, e], scalar=gain[:, t:t + 1],
+                                                   in1=live["sig", c, u, e][:], op0=ALU.mult, op1=ALU.add)
+                return
             for e in range(2):
                 t = 2 * u + e
                 nc.vector.tensor_tensor(out=live["sum", c][:, t, :], in0=live["sig", c, u, e][:], in1=live["sum", c][:, t, :], op=ALU.add)
@@ -248,7 +262,11 @@ def tile_brainquantumlayer_pa_t_kernel(tc, x, W_in, b_in, weights, J, theta, lam
                 live["out", c] = work.tile([P, SUB, D], F32, name="out_sb", bufs=2)
             bank = psum.tile([P, PACK, P], F32, name="bank_o", tag="to_scalar", bufs=3)
             for t in range(PACK):
-                nc.tensor.transpose(out=bank[:, t, :], in_=live["sum", c][:, t, P * s:P * (s + 1)], identity=ident[:])
+                rows = slice(P * s, P * (s + 1))
+                parts = [live["sum", c], live["sum2", c]] if c in MIXED else [live["sum", c]]
+                for i, part in enumerate(parts):
+                    nc.tensor.matmul(out=bank[:, t, :], lhsT=part[:, t, rows], rhs=ident[:], is_transpose=True,
+                                     start=(i == 0), stop=(i == len(parts) - 1))
             nc.scalar.activation(out=live["out", c][:, s, :].rearrange("p (u q e) -> p u q e", u=2, q=P, e=2),
                                  in_=bank[:].rearrange("p (u e) q -> p u q e", u=2, e=2), func=ACT.Tanh)
             if c == NCH - 1:

@@ -131,8 +131,11 @@ def tile_brainquantumlayer_pa_t_kernel(tc, x, W_in, b_in, weights, J, theta, lam
             nc.tensor.matmul_mx(out=acc[:], lhsT=stationary[0][:, cols].bitcast(FP8X4), lhsT_scale=stationary[1][:, cols],
                                 rhs=moving[0][:].bitcast(FP8X4), rhs_scale=moving[1][:], start=True, stop=True)
 
+        def regrouped_tile(name):
+            return work.tile([P, PACK * CH], BF16, name=name, bufs=1, align_bytes=64)
+
         def regroup(planes, name, on_vector):
-            grouped = work.tile([P, PACK * CH], BF16, name=name, bufs=1, align_bytes=64)
+            grouped = regrouped_tile(name)
             if on_vector:
                 nc.vector.tensor_copy(out=grouped[:].rearrange("p (c i t) -> p c t i", i=4, t=PACK),
                                       in_=planes[:].rearrange("p t (c i) -> p c t i", i=4))
@@ -169,7 +172,7 @@ def tile_brainquantumlayer_pa_t_kernel(tc, x, W_in, b_in, weights, J, theta, lam
 
         def project(c, t):
             if t == 0:
-                live["state", c] = work.tile([P, PACK, CH], BF16, name="state_pl", bufs=2)
+                live["state", c] = work.tile([P, PACK, CH], BF16, name="state_pl", bufs=3)
                 live["s", c] = work.tile([P, PACK, CH], F32, name="s_pl", bufs=4)
             acc = psum.tile([P, CH], F32, name="acc_state", tag="to_scalar", bufs=3)
             mx_pass(acc, live["w_in"], t, live["xq", c])
@@ -183,7 +186,7 @@ def tile_brainquantumlayer_pa_t_kernel(tc, x, W_in, b_in, weights, J, theta, lam
             nc.scalar.activation(out=live["state", c][:, t, :], in_=acc[:], func=ACT.Identity, bias=b_f[:, t:t + 1], scale=1.0)
 
         def project_first():
-            live["state", 0] = work.tile([P, PACK, CH], BF16, name="state_pl", bufs=2)
+            live["state", 0] = work.tile([P, PACK, CH], BF16, name="state_pl", bufs=3)
             live["s", 0] = work.tile([P, PACK, CH], F32, name="s_pl", bufs=4)
             accs = []
             for t in range(PACK):
@@ -301,7 +304,7 @@ def tile_brainquantumlayer_pa_t_kernel(tc, x, W_in, b_in, weights, J, theta, lam
             planes = 2 * h + 12
             do(add_delta, c, u)
             do(recurrent, *nxt)
-            project_up_to(planes - 1)
+            project_up_to(planes if u == 0 else planes - 1)
             do(add_noise, c, u)
             do(transpose_noise, *nxt)
             do(finish, c - 1, 2 * u)
@@ -327,33 +330,43 @@ def tile_brainquantumlayer_pa_t_kernel(tc, x, W_in, b_in, weights, J, theta, lam
                 leave_s(0, t, accs[t])
             leave_state(0, 0, accs[0])
             transpose_both(1)
+            do(transpose_noise, 0, 0)
             for t in range(1, PACK):
                 leave_state(0, t, accs[t])
             transpose_both(2)
             do(regroup_s, 0)
+            do(quantise_x, 1)
             do(quantise_s, 0)
             do(recurrent, 0, 0)
-            do(transpose_noise, 0, 0)
-            do(quantise_x, 1)
-            do(quantise_x, 2)
-            project_up_to(2 * PACK + 2)
-            mask_weights(w_sb, "w_g")
-            live["w"] = quantise(live["w_g"], "w_q", keep)
-            do(regroup_state, 0)
-            do(quantise_state, 0)
-            do(signal, 0, 0)
+            project_up_to(PACK + 2)
             do(add_delta, 0, 0)
             do(recurrent, 0, 1)
             do(add_noise, 0, 0)
             do(transpose_noise, 0, 1)
+            project_up_to(2 * PACK)
+            mask_weights(w_sb, "w_g")
+            do(quantise_x, 2)
+            project_up_to(2 * PACK + 2)
+            live["w"] = quantise(live["w_g"], "w_q", keep)
+            do(regroup_state, 0)
+            do(quantise_state, 0)
+            do(signal, 0, 0)
             transpose_both(3)
             project_up_to(3 * PACK)
+            do(add_delta, 0, 1)
+            do(add_noise, 0, 1)
+            do(transpose_noise, 1, 0)
             do(regroup_s, 1)
-            do(quantise_s, 1)
+            do(add_signal, 0, 0)
+            do(signal, 0, 1)
             do(regroup_state, 1)
-            do(quantise_state, 1)
             do(quantise_x, 3)
+            do(quantise_state, 1)
+            do(quantise_s, 1)
+            do(recurrent, 1, 0)
+            do(add_signal, 0, 1)
+            do(signal, 1, 0)
 
-        for c in range(NCH + 1):
-            half_step(c, 0)
-            half_step(c, 1)
+            for c in range(NCH + 1):
+                half_step(c, 0)
+                half_step(c, 1)

@@ -19,12 +19,14 @@ M, D = 4096, 512
 CH = 512
 NCH = M // CH
 SUB = CH // P
+HALF = CH // 2
 FLOPS = 3 * 2 * M * D * D
 
 PI_HI = 3.1415927410125732
 PI_LO = math.pi - PI_HI
 HURRIED = 2
 MIXED = (NCH - 2, NCH - 1)
+HALVED = (NCH - 2, NCH - 1)
 
 
 def tile_brainquantumlayer_pa_t_kernel(tc, x, W_in, b_in, weights, J, theta, lam, mask, noise_raw, out):
@@ -126,10 +128,10 @@ def tile_brainquantumlayer_pa_t_kernel(tc, x, W_in, b_in, weights, J, theta, lam
             nc.vector.quantize_mx(out=codes[:].bitcast(FP8X4), scales=scales[:], in_=grouped[:])
             return codes, scales
 
-        def mx_pass(acc, stationary, t, moving):
+        def mx_pass(acc, stationary, t, moving, rows=slice(0, CH)):
             cols = slice(P * t, P * (t + 1))
-            nc.tensor.matmul_mx(out=acc[:], lhsT=stationary[0][:, cols].bitcast(FP8X4), lhsT_scale=stationary[1][:, cols],
-                                rhs=moving[0][:].bitcast(FP8X4), rhs_scale=moving[1][:], start=True, stop=True)
+            nc.tensor.matmul_mx(out=acc, lhsT=stationary[0][:, cols].bitcast(FP8X4), lhsT_scale=stationary[1][:, cols],
+                                rhs=moving[0][:, rows].bitcast(FP8X4), rhs_scale=moving[1][:, rows], start=True, stop=True)
 
         def regrouped_tile(name):
             return work.tile([P, PACK * CH], BF16, name=name, bufs=1, align_bytes=64)
@@ -175,7 +177,7 @@ def tile_brainquantumlayer_pa_t_kernel(tc, x, W_in, b_in, weights, J, theta, lam
                 live["state", c] = work.tile([P, PACK, CH], BF16, name="state_pl", bufs=3)
                 live["s", c] = work.tile([P, PACK, CH], F32, name="s_pl", bufs=4)
             acc = psum.tile([P, CH], F32, name="acc_state", tag="to_scalar", bufs=3)
-            mx_pass(acc, live["w_in"], t, live["xq", c])
+            mx_pass(acc[:], live["w_in"], t, live["xq", c])
             leave_s(c, t, acc)
             leave_state(c, t, acc)
 
@@ -191,7 +193,7 @@ def tile_brainquantumlayer_pa_t_kernel(tc, x, W_in, b_in, weights, J, theta, lam
             accs = []
             for t in range(PACK):
                 acc = psum.tile([P, CH], F32, name="acc_first", tag="acc_rec" if t < 2 else "acc_sig", bufs=2)
-                mx_pass(acc, live["w_in"], t, live["xq", 0])
+                mx_pass(acc[:], live["w_in"], t, live["xq", 0])
                 accs.append(acc)
             for t in range(PACK):
                 done.add((project, 0, (t,)))
@@ -209,22 +211,30 @@ def tile_brainquantumlayer_pa_t_kernel(tc, x, W_in, b_in, weights, J, theta, lam
         def quantise_state(c):
             live["stq", c] = quantise(live["state_g", c], "state_q", work)
 
+        def half_rows(h):
+            return slice(HALF * h, HALF * (h + 1))
+
+        def product(name, tag, c, u, stationary, moving):
+            for v in range(2):
+                acc = psum.tile([P, 2, HALF], F32, name="acc_" + name, tag=tag, bufs=2)
+                if c in HALVED:
+                    for e in range(2):
+                        mx_pass(acc[:, e, :], stationary, 2 * v + e, moving, half_rows(u))
+                else:
+                    mx_pass(acc[:].rearrange("p h m -> p (h m)"), stationary, 2 * u + v, moving)
+                live[name, c, u, v] = acc
+
         def recurrent(c, u):
-            for e in range(2):
-                acc = psum.tile([P, CH], F32, name="acc_rec", tag="acc_rec", bufs=2)
-                mx_pass(acc, live["j"], 2 * u + e, live["sq", c])
-                live["rec", c, u, e] = acc
+            product("rec", "acc_rec", c, u, live["j"], live["sq", c])
 
         def signal(c, u):
-            for e in range(2):
-                acc = psum.tile([P, CH], F32, name="acc_sig", tag="acc_sig", bufs=2)
-                mx_pass(acc, live["w"], 2 * u + e, live["stq", c])
-                live["sig", c, u, e] = acc
+            product("sig", "acc_sig", c, u, live["w"], live["stq", c])
 
         def transpose_noise(c, u):
             bank = psum.tile([P, CH], F32, name="bank_n", bufs=1)
-            for s in range(SUB):
-                nc.tensor.transpose(out=bank[:, P * s:P * (s + 1)], in_=n_sb[c][:, s, :].bitcast(F32)[:, P * u:P * (u + 1)], identity=ident[:])
+            for i in range(SUB):
+                s, v = (2 * u + i % 2, i // 2) if c in HALVED else (i, u)
+                nc.tensor.transpose(out=bank[:, P * i:P * (i + 1)], in_=n_sb[c][:, s, :].bitcast(F32)[:, P * v:P * (v + 1)], identity=ident[:])
             if c in MIXED:
                 words = work.tile([P, CH], F32, name="noise_sb", bufs=3)
                 nc.scalar.copy(out=words[:], in_=bank[:])
@@ -234,10 +244,14 @@ def tile_brainquantumlayer_pa_t_kernel(tc, x, W_in, b_in, weights, J, theta, lam
         def add_delta(c, u):
             if u == 0:
                 live["sum", c] = work.tile([P, PACK, CH], F32, name="sum_pl", bufs=3)
-            for e in range(2):
-                t = 2 * u + e
-                nc.vector.scalar_tensor_tensor(out=live["sum", c][:, t, :], in0=live["rec", c, u, e][:], scalar=lam_f[:, 0:1],
-                                               in1=live["s", c][:, t, :], op0=ALU.mult, op1=ALU.mult)
+            for v in range(2):
+                acc = live["rec", c, u, v]
+                if c in HALVED:
+                    part, acc = (slice(None), slice(2 * v, 2 * v + 2), half_rows(u)), acc[:]
+                else:
+                    part, acc = (slice(None), 2 * u + v, slice(None)), acc[:].rearrange("p h m -> p (h m)")
+                nc.vector.scalar_tensor_tensor(out=live["sum", c][part], in0=acc, scalar=lam_f[:, 0:1],
+                                               in1=live["s", c][part], op0=ALU.mult, op1=ALU.mult)
 
         def add_noise(c, u):
             if c in MIXED:
@@ -248,17 +262,22 @@ def tile_brainquantumlayer_pa_t_kernel(tc, x, W_in, b_in, weights, J, theta, lam
                                                in1=live["sum", c][:, t, :], op0=ALU.mult, op1=ALU.add)
 
         def add_signal(c, u):
-            if c in MIXED:
-                if u == 0:
-                    live["sum2", c] = work.tile([P, PACK, CH], F32, name="sum2_pl", bufs=2)
+            if c not in MIXED:
                 for e in range(2):
                     t = 2 * u + e
-                    nc.vector.scalar_tensor_tensor(out=live["sum2", c][:, t, :], in0=live["noise", c, u][:, :, e], scalar=gain[:, t:t + 1],
-                                                   in1=live["sig", c, u, e][:], op0=ALU.mult, op1=ALU.add)
+                    nc.vector.tensor_tensor(out=live["sum", c][:, t, :], in0=live["sig", c, u, e][:].rearrange("p h m -> p (h m)"),
+                                            in1=live["sum", c][:, t, :], op=ALU.add)
                 return
-            for e in range(2):
-                t = 2 * u + e
-                nc.vector.tensor_tensor(out=live["sum", c][:, t, :], in0=live["sig", c, u, e][:], in1=live["sum", c][:, t, :], op=ALU.add)
+            if u == 0:
+                live["sum2", c] = work.tile([P, PACK, CH], F32, name="sum2_pl", bufs=2)
+            noise = live["noise", c, u]
+            for t in range(PACK) if c in HALVED else (2 * u, 2 * u + 1):
+                v, e = t // 2, t % 2
+                if c in HALVED:
+                    out_ap, noise_ap, sig_ap = live["sum2", c][:, t, half_rows(u)], noise[:, half_rows(v), e], live["sig", c, u, v][:, e, :]
+                else:
+                    out_ap, noise_ap, sig_ap = live["sum2", c][:, t, :], noise[:, :, e], live["sig", c, u, e][:].rearrange("p h m -> p (h m)")
+                nc.vector.scalar_tensor_tensor(out=out_ap, in0=noise_ap, scalar=gain[:, t:t + 1], in1=sig_ap, op0=ALU.mult, op1=ALU.add)
 
         def finish(c, s):
             if s == 0:
@@ -291,24 +310,39 @@ def tile_brainquantumlayer_pa_t_kernel(tc, x, W_in, b_in, weights, J, theta, lam
             do(transpose_x, c, 1)
 
         def quantise_both(c):
-            do(quantise_s, c)
             do(quantise_state, c)
+            do(quantise_s, c)
 
         def regroup_both(n):
             do(regroup_s, n // PACK - 1)
             do(regroup_state, n // PACK - 1)
 
+        def finish_due(c, u):
+            if c - 1 not in HALVED:
+                pairs = [(c - 1, u)]
+            else:
+                pairs = [(c - 1, 1)]
+            if c in HALVED and u == 1:
+                pairs.append((c, 0))
+            for chunk, pair in pairs:
+                do(finish, chunk, 2 * pair)
+                do(finish, chunk, 2 * pair + 1)
+
         def half_step(c, u):
             h = 2 * c + u
             nxt = (c, 1) if u == 0 else (c + 1, 0)
             planes = 2 * h + 12
+            if (c >= NCH - 2):
+                do(transpose_noise, *nxt)
+            if (c >= NCH - 2 or u == 1):
+                finish_due(c, u)
             do(add_delta, c, u)
             do(recurrent, *nxt)
             project_up_to(planes if u == 0 else planes - 1)
             do(add_noise, c, u)
             do(transpose_noise, *nxt)
-            do(finish, c - 1, 2 * u)
-            do(finish, c - 1, 2 * u + 1)
+            if not (c >= NCH - 2 or u == 1):
+                finish_due(c, u)
             do(transpose_x, c + 4, u)
             do(add_signal, c, u)
             do(signal, *nxt)
@@ -318,7 +352,7 @@ def tile_brainquantumlayer_pa_t_kernel(tc, x, W_in, b_in, weights, J, theta, lam
                 quantise_both(c + 1)
             regroup_both(planes)
 
-        with tc.manual_schedule(engines={mybir.EngineType.PE, mybir.EngineType.Activation, mybir.EngineType.DVE}):
+        with tc.manual_schedule(engines={mybir.EngineType.PE, mybir.EngineType.Activation, mybir.EngineType.DVE, mybir.EngineType.Pool}):
             prepare_w_in()
             transpose_both(0)
             quantise_w_in()

@@ -309,14 +309,6 @@ def tile_brainquantumlayer_pa_t_kernel(tc, x, W_in, b_in, weights, J, theta, lam
             do(transpose_x, c, 0)
             do(transpose_x, c, 1)
 
-        def quantise_both(c):
-            do(quantise_state, c)
-            do(quantise_s, c)
-
-        def regroup_both(n):
-            do(regroup_s, n // PACK - 1)
-            do(regroup_state, n // PACK - 1)
-
         def finish_due(c, u):
             if c - 1 not in HALVED:
                 pairs = [(c - 1, u)]
@@ -329,28 +321,32 @@ def tile_brainquantumlayer_pa_t_kernel(tc, x, W_in, b_in, weights, J, theta, lam
                 do(finish, chunk, 2 * pair + 1)
 
         def half_step(c, u):
-            h = 2 * c + u
             nxt = (c, 1) if u == 0 else (c + 1, 0)
-            planes = 2 * h + 12
-            if (c >= NCH - 2):
+            tail = c >= NCH - 2
+            if tail:
                 do(transpose_noise, *nxt)
-            if (c >= NCH - 2 or u == 1):
+            if tail or u == 1:
                 finish_due(c, u)
             do(add_delta, c, u)
+            if u == 1:
+                if c > 0:
+                    do(quantise_x, c + 3)
+                    do(quantise_state, c + 1)
+                    do(quantise_s, c + 1)
+                do(regroup_s, c + 2)
+                do(regroup_state, c + 2)
             do(recurrent, *nxt)
-            project_up_to(planes if u == 0 else planes - 1)
+            if u == 0:
+                project_up_to(PACK * (c + 3))
             do(add_noise, c, u)
             do(transpose_noise, *nxt)
-            if not (c >= NCH - 2 or u == 1):
+            if not (tail or u == 1):
                 finish_due(c, u)
             do(transpose_x, c + 4, u)
             do(add_signal, c, u)
             do(signal, *nxt)
-            project_up_to(planes)
-            if u == 0 and c > 0:
-                do(quantise_x, c + 3)
-                quantise_both(c + 1)
-            regroup_both(planes)
+            if u == 1:
+                project_up_to(PACK * (c + 3) + 2)
 
         with tc.manual_schedule(engines={mybir.EngineType.PE, mybir.EngineType.Activation, mybir.EngineType.DVE, mybir.EngineType.Pool}):
             prepare_w_in()
@@ -397,10 +393,13 @@ def tile_brainquantumlayer_pa_t_kernel(tc, x, W_in, b_in, weights, J, theta, lam
             do(quantise_x, 3)
             do(quantise_state, 1)
             do(quantise_s, 1)
+            do(regroup_s, 2)
+            do(regroup_state, 2)
             do(recurrent, 1, 0)
             do(add_signal, 0, 1)
             do(signal, 1, 0)
 
+        with tc.manual_schedule(engines={mybir.EngineType.DVE, mybir.EngineType.Pool}):
             for c in range(NCH + 1):
                 half_step(c, 0)
                 half_step(c, 1)

@@ -24,7 +24,7 @@ FLOPS = 3 * 2 * M * D * D
 
 PI_HI = 3.1415927410125732
 PI_LO = math.pi - PI_HI
-HURRIED = 2
+SWAPPED = 1
 MIXED = (NCH - 2, NCH - 1)
 HALVED = (NCH - 2, NCH - 1)
 
@@ -49,13 +49,10 @@ def tile_brainquantumlayer_pa_t_kernel(tc, x, W_in, b_in, weights, J, theta, lam
             nc.scalar.dma_start(out=dst[:].rearrange("p (u e) -> p u e", u=2),
                                 in_=v.rearrange("(u p e) -> p u e", u=2, p=P, e=2))
 
-        b_bf = keep.tile([P, PACK], BF16, name="b_bf")
         th_bf = keep.tile([P, PACK], BF16, name="th_bf")
         lam_bf = keep.tile([P, 1], BF16, name="lam_bf")
-        with nc.allow_non_contiguous_dma(reason="three small vectors, once"):
+        with nc.allow_non_contiguous_dma(reason="one small vector, once"):
             load_vector(th_bf, theta)
-            load_vector(b_bf, b_in)
-            nc.scalar.dma_start(out=lam_bf[:], in_=lam.partition_broadcast(P))
 
         w_in_sb = keep.tile([P, PACK, D], BF16, name="w_in_sb")
         load_planes(w_in_sb, W_in)
@@ -63,12 +60,17 @@ def tile_brainquantumlayer_pa_t_kernel(tc, x, W_in, b_in, weights, J, theta, lam
         n_sb = [keep.tile([P, SUB, D], BF16, name="n_sb%d" % c) for c in range(NCH)]
         for h in range(2):
             nc.sync.dma_start(out=x_sb[0][:, 2 * h:2 * h + 2, :], in_=x_v[0][:, 2 * h:2 * h + 2, :])
+        b_rows = keep.tile([P, P], F32, name="b_rows")
+        nc.vector.memset(b_rows[:], 0.0)
+        nc.sync.dma_start(out=b_rows[0:2, :].bitcast(BF16), in_=b_in.rearrange("(u w) -> u w", u=2))
         j_sb = keep.tile([P, PACK, D], BF16, name="j_sb")
         m_sb = keep.tile([P, PACK, D], BF16, name="m_sb")
         w_sb = keep.tile([P, PACK, D], BF16, name="w_sb")
         load_planes(j_sb, J)
         load_planes(m_sb, mask)
         load_planes(w_sb, weights)
+        with nc.allow_non_contiguous_dma(reason="one value to each partition, once"):
+            nc.sync.dma_start(out=lam_bf[:], in_=lam.partition_broadcast(P))
         for c in range(NCH):
             if c + 1 < NCH:
                 nc.sync.dma_start(out=x_sb[c + 1][:], in_=x_v[c + 1])
@@ -95,19 +97,17 @@ def tile_brainquantumlayer_pa_t_kernel(tc, x, W_in, b_in, weights, J, theta, lam
         nc.scalar.activation(out=first_tanh[:], in_=sin_y[:], func=ACT.Tanh)
         gain = keep.tile([P, PACK], F32, name="gain")
         nc.scalar.activation(out=gain[:], in_=sin_y[:], func=ACT.Abs, scale=0.1)
-        b_f = keep.tile([P, PACK], F32, name="b_f")
-        nc.vector.tensor_copy(out=b_f[:], in_=b_bf[:])
-        lam_f = keep.tile([P, 1], F32, name="lam_f")
-        nc.vector.tensor_copy(out=lam_f[:], in_=lam_bf[:])
+        b_words = keep.tile([P, 2], F32, name="b_words")
+        b_bf = b_words[:].bitcast(BF16)
 
         done = set()
         live = {}
 
         def grouped_tile():
-            return work.tile([P, PACK * D], BF16, name="grouped", tag="grouped", bufs=5, align_bytes=64)
+            return work.tile([P, PACK * D], BF16, name="grouped", tag="grouped", bufs=4, align_bytes=64)
 
         def transpose_words(rows, h):
-            bank = psum.tile([P, 2, 2 * P], F32, name="bank_w", tag="to_scalar", bufs=3)
+            bank = psum.tile([P, 2, 2 * P], F32, name="bank_w", tag="to_scalar", bufs=4)
             for i in range(2):
                 words = rows[:, 2 * h + i, :].bitcast(F32)
                 for v in range(2):
@@ -122,29 +122,42 @@ def tile_brainquantumlayer_pa_t_kernel(tc, x, W_in, b_in, weights, J, theta, lam
             else:
                 nc.scalar.copy(out=dst, in_=src)
 
+        def operand_tiles(name, pool, operands=1):
+            return (pool.tile([P, operands * D], U32, name=name + "_c", align_bytes=64),
+                    pool.tile([P, operands * D], U8, name=name + "_s", align_bytes=64))
+
+        def one_operand(tiles, i):
+            return tiles[0][:, D * i:D * (i + 1)], tiles[1][:, D * i:D * (i + 1)]
+
+        def quantise_into(operand, grouped):
+            nc.vector.quantize_mx(out=operand[0][:].bitcast(FP8X4), scales=operand[1][:], in_=grouped[:])
+
         def quantise(grouped, name, pool):
-            codes = pool.tile([P, D], U32, name=name + "_c", align_bytes=64)
-            scales = pool.tile([P, D], U8, name=name + "_s", align_bytes=64)
-            nc.vector.quantize_mx(out=codes[:].bitcast(FP8X4), scales=scales[:], in_=grouped[:])
-            return codes, scales
+            operand = operand_tiles(name, pool)
+            quantise_into(operand, grouped)
+            return operand
 
         def mx_pass(acc, stationary, t, moving, rows=slice(0, CH)):
             cols = slice(P * t, P * (t + 1))
             nc.tensor.matmul_mx(out=acc, lhsT=stationary[0][:, cols].bitcast(FP8X4), lhsT_scale=stationary[1][:, cols],
                                 rhs=moving[0][:, rows].bitcast(FP8X4), rhs_scale=moving[1][:, rows], start=True, stop=True)
 
-        def regrouped_tile(name):
-            return work.tile([P, PACK * CH], BF16, name=name, bufs=1, align_bytes=64)
+        def regrouped_tile(tag, operands=1):
+            return work.tile([P, operands * PACK * CH], BF16, name="regrouped", tag=tag, bufs=1, align_bytes=64)
 
-        def regroup(planes, name, on_vector):
-            grouped = regrouped_tile(name)
+        def regroup(planes, grouped, on_vector):
             if on_vector:
-                nc.vector.tensor_copy(out=grouped[:].rearrange("p (c i t) -> p c t i", i=4, t=PACK),
+                nc.vector.tensor_copy(out=grouped.rearrange("p (c i t) -> p c t i", i=4, t=PACK),
                                       in_=planes[:].rearrange("p t (c i) -> p c t i", i=4))
             else:
-                nc.gpsimd.tensor_scalar(out=grouped[:].rearrange("p (m t) -> p m t", t=PACK), in0=planes[:].rearrange("p t m -> p m t"),
+                nc.gpsimd.tensor_scalar(out=grouped.rearrange("p (c i t) -> p c t i", i=4, t=PACK),
+                                        in0=planes[:].rearrange("p t (c i) -> p c t i", i=4),
                                         scalar1=1.0, scalar2=0.0, op0=ALU.mult, op1=ALU.add)
-            return grouped
+
+        def spread_b():
+            bank = psum.tile([P, P], F32, name="bank_b", tag="to_scalar", bufs=4)
+            nc.tensor.transpose(out=bank[:], in_=b_rows[:], identity=ident[:])
+            nc.vector.tensor_copy(out=b_words[:], in_=bank[:, 0:2])
 
         def prepare_w_in():
             grouped = grouped_tile()
@@ -155,14 +168,15 @@ def tile_brainquantumlayer_pa_t_kernel(tc, x, W_in, b_in, weights, J, theta, lam
         def quantise_w_in():
             live["w_in"] = quantise(live["w_in_g"], "w_in_q", keep)
 
-        def mask_weights(w, name):
-            grouped = grouped_tile()
-            g_v = grouped[:].rearrange("p (u e q t) -> p u e q t", u=2, e=2, q=P, t=PACK)
+        def mask_weights(w):
+            nc.vector.tensor_tensor(out=w[:], in0=w[:], in1=m_sb[:], op=ALU.mult)
+
+        def group_weights(w, name):
+            live[name] = grouped_tile()
+            g_v = live[name][:].rearrange("p (u e q t) -> p u e q t", u=2, e=2, q=P, t=PACK)
             w_v = w[:].rearrange("p t (u q e) -> p u e q t", u=2, q=P, e=2)
-            m_v = m_sb[:].rearrange("p t (u q e) -> p u e q t", u=2, q=P, e=2)
             for e in range(2):
-                nc.vector.tensor_tensor(out=g_v[:, :, e, :, :], in0=w_v[:, :, e, :, :], in1=m_v[:, :, e, :, :], op=ALU.mult)
-            live[name] = grouped
+                nc.vector.tensor_copy(out=g_v[:, :, e, :, :], in_=w_v[:, :, e, :, :])
 
         def transpose_x(c, h):
             if h == 0:
@@ -176,23 +190,23 @@ def tile_brainquantumlayer_pa_t_kernel(tc, x, W_in, b_in, weights, J, theta, lam
             if t == 0:
                 live["state", c] = work.tile([P, PACK, CH], BF16, name="state_pl", bufs=3)
                 live["s", c] = work.tile([P, PACK, CH], F32, name="s_pl", bufs=4)
-            acc = psum.tile([P, CH], F32, name="acc_state", tag="to_scalar", bufs=3)
+            acc = psum.tile([P, CH], F32, name="acc_state", tag="to_scalar", bufs=4)
             mx_pass(acc[:], live["w_in"], t, live["xq", c])
             leave_s(c, t, acc)
             leave_state(c, t, acc)
 
         def leave_s(c, t, acc):
-            nc.scalar.activation(out=live["s", c][:, t, :], in_=acc[:], func=ACT.Tanh, bias=b_f[:, t:t + 1], scale=1.0)
+            nc.scalar.activation(out=live["s", c][:, t, :], in_=acc[:], func=ACT.Tanh, bias=b_bf[:, t:t + 1], scale=1.0)
 
         def leave_state(c, t, acc):
-            nc.scalar.activation(out=live["state", c][:, t, :], in_=acc[:], func=ACT.Identity, bias=b_f[:, t:t + 1], scale=1.0)
+            nc.scalar.activation(out=live["state", c][:, t, :], in_=acc[:], func=ACT.Identity, bias=b_bf[:, t:t + 1], scale=1.0)
 
         def project_first():
             live["state", 0] = work.tile([P, PACK, CH], BF16, name="state_pl", bufs=3)
             live["s", 0] = work.tile([P, PACK, CH], F32, name="s_pl", bufs=4)
             accs = []
             for t in range(PACK):
-                acc = psum.tile([P, CH], F32, name="acc_first", tag="acc_rec" if t < 2 else "acc_sig", bufs=2)
+                acc = psum.tile([P, CH], F32, name="acc_first", tag="to_vector", bufs=4)
                 mx_pass(acc[:], live["w_in"], t, live["xq", 0])
                 accs.append(acc)
             for t in range(PACK):
@@ -200,38 +214,52 @@ def tile_brainquantumlayer_pa_t_kernel(tc, x, W_in, b_in, weights, J, theta, lam
             return accs
 
         def regroup_s(c):
-            live["s_g", c] = regroup(live["s", c], "s_g", on_vector=(c < HURRIED))
+            live["s_g", c] = regrouped_tile("state_g" if c == SWAPPED else "s_g")
+            regroup(live["s", c], live["s_g", c][:], on_vector=(c == 0))
 
         def regroup_state(c):
-            live["state_g", c] = regroup(live["state", c], "state_g", on_vector=(c < HURRIED))
+            live["state_g", c] = regrouped_tile("s_g" if c == SWAPPED else "state_g")
+            regroup(live["state", c], live["state_g", c][:], on_vector=True)
 
         def quantise_s(c):
-            live["sq", c] = quantise(live["s_g", c], "s_q", work)
+            live["both_q", c] = operand_tiles("both_q", work, operands=2)
+            live["sq", c] = one_operand(live["both_q", c], 0)
+            quantise_into(live["sq", c], live["s_g", c])
 
         def quantise_state(c):
-            live["stq", c] = quantise(live["state_g", c], "state_q", work)
+            live["stq", c] = one_operand(live["both_q", c], 1)
+            quantise_into(live["stq", c], live["state_g", c])
+
+        def regroup_both(c):
+            live["both_g", c] = regrouped_tile("s_g", operands=2)
+            for i, planes in enumerate((live["s", c], live["state", c])):
+                regroup(planes, live["both_g", c][:, PACK * CH * i:PACK * CH * (i + 1)], on_vector=False)
+
+        def quantise_both(c):
+            tiles = operand_tiles("both_q", work, operands=2)
+            quantise_into(tiles, live["both_g", c])
+            live["sq", c], live["stq", c] = one_operand(tiles, 0), one_operand(tiles, 1)
 
         def half_rows(h):
             return slice(HALF * h, HALF * (h + 1))
 
-        def product(name, tag, c, u, stationary, moving):
-            for v in range(2):
-                acc = psum.tile([P, 2, HALF], F32, name="acc_" + name, tag=tag, bufs=2)
-                if c in HALVED:
-                    for e in range(2):
-                        mx_pass(acc[:, e, :], stationary, 2 * v + e, moving, half_rows(u))
-                else:
-                    mx_pass(acc[:].rearrange("p h m -> p (h m)"), stationary, 2 * u + v, moving)
-                live[name, c, u, v] = acc
+        def product(name, c, u, v, stationary, moving):
+            acc = psum.tile([P, 2, HALF], F32, name="acc_" + name, tag="to_vector", bufs=4)
+            if c in HALVED:
+                for e in range(2):
+                    mx_pass(acc[:, e, :], stationary, 2 * v + e, moving, half_rows(u))
+            else:
+                mx_pass(acc[:].rearrange("p h m -> p (h m)"), stationary, 2 * u + v, moving)
+            live[name, c, u, v] = acc
 
-        def recurrent(c, u):
-            product("rec", "acc_rec", c, u, live["j"], live["sq", c])
+        def recurrent(c, u, v):
+            product("rec", c, u, v, live["j"], live["sq", c])
 
-        def signal(c, u):
-            product("sig", "acc_sig", c, u, live["w"], live["stq", c])
+        def signal(c, u, v):
+            product("sig", c, u, v, live["w"], live["stq", c])
 
         def transpose_noise(c, u):
-            bank = psum.tile([P, CH], F32, name="bank_n", bufs=1)
+            bank = psum.tile([P, CH], F32, name="bank_n", tag="to_vector", bufs=4)
             for i in range(SUB):
                 s, v = (2 * u + i % 2, i // 2) if c in HALVED else (i, u)
                 nc.tensor.transpose(out=bank[:, P * i:P * (i + 1)], in_=n_sb[c][:, s, :].bitcast(F32)[:, P * v:P * (v + 1)], identity=ident[:])
@@ -250,7 +278,7 @@ def tile_brainquantumlayer_pa_t_kernel(tc, x, W_in, b_in, weights, J, theta, lam
                     part, acc = (slice(None), slice(2 * v, 2 * v + 2), half_rows(u)), acc[:]
                 else:
                     part, acc = (slice(None), 2 * u + v, slice(None)), acc[:].rearrange("p h m -> p (h m)")
-                nc.vector.scalar_tensor_tensor(out=live["sum", c][part], in0=acc, scalar=lam_f[:, 0:1],
+                nc.vector.scalar_tensor_tensor(out=live["sum", c][part], in0=acc, scalar=lam_bf[:, 0:1],
                                                in1=live["s", c][part], op0=ALU.mult, op1=ALU.mult)
 
         def add_noise(c, u):
@@ -282,7 +310,7 @@ def tile_brainquantumlayer_pa_t_kernel(tc, x, W_in, b_in, weights, J, theta, lam
         def finish(c, s):
             if s == 0:
                 live["out", c] = work.tile([P, SUB, D], F32, name="out_sb", bufs=2)
-            bank = psum.tile([P, PACK, P], F32, name="bank_o", tag="to_scalar", bufs=3)
+            bank = psum.tile([P, PACK, P], F32, name="bank_o", tag="to_scalar", bufs=4)
             for t in range(PACK):
                 rows = slice(P * s, P * (s + 1))
                 parts = [live["sum", c], live["sum2", c]] if c in MIXED else [live["sum", c]]
@@ -316,90 +344,100 @@ def tile_brainquantumlayer_pa_t_kernel(tc, x, W_in, b_in, weights, J, theta, lam
                 pairs = [(c - 1, 1)]
             if c in HALVED and u == 1:
                 pairs.append((c, 0))
-            for chunk, pair in pairs:
-                do(finish, chunk, 2 * pair)
-                do(finish, chunk, 2 * pair + 1)
+            return [(finish, chunk, 2 * pair + i) for chunk, pair in pairs for i in range(2)]
 
         def half_step(c, u):
             nxt = (c, 1) if u == 0 else (c + 1, 0)
+            made = PACK * (c + 3) if u == 0 else PACK * (c + 3) + 2
+            planes = [(project, i // PACK, i % PACK) for i in range(made - 2, made)]
+            x_half = [(transpose_x, c + 4, u)]
+            rows = finish_due(c, u)
+            items = planes + rows + x_half if u == 0 else rows + x_half + planes
             tail = c >= NCH - 2
+            early = len(rows) if tail else 0
             if tail:
-                do(transpose_noise, *nxt)
-            if tail or u == 1:
-                finish_due(c, u)
+                items = rows + planes + x_half
             do(add_delta, c, u)
+            do(signal, c, u, 1)
+            for item in items[:early]:
+                do(*item)
             if u == 1:
                 if c > 0:
                     do(quantise_x, c + 3)
-                    do(quantise_state, c + 1)
-                    do(quantise_s, c + 1)
-                do(regroup_s, c + 2)
-                do(regroup_state, c + 2)
-            do(recurrent, *nxt)
-            if u == 0:
-                project_up_to(PACK * (c + 3))
+                    do(quantise_both, c + 1)
+                do(regroup_both, c + 2)
+            do(recurrent, *nxt, 0)
+            for item in items[early:2]:
+                do(*item)
             do(add_noise, c, u)
-            do(transpose_noise, *nxt)
-            if not (tail or u == 1):
-                finish_due(c, u)
-            do(transpose_x, c + 4, u)
+            do(recurrent, *nxt, 1)
+            for item in items[max(early, 2):4]:
+                do(*item)
             do(add_signal, c, u)
-            do(signal, *nxt)
-            if u == 1:
-                project_up_to(PACK * (c + 3) + 2)
+            do(transpose_noise, *nxt)
+            do(signal, *nxt, 0)
+            for item in items[max(early, 4):]:
+                do(*item)
+
 
         with tc.manual_schedule(engines={mybir.EngineType.PE, mybir.EngineType.Activation, mybir.EngineType.DVE, mybir.EngineType.Pool}):
             prepare_w_in()
             transpose_both(0)
+            spread_b()
             quantise_w_in()
             do(quantise_x, 0)
             accs = project_first()
-            mask_weights(j_sb, "j_g")
+            mask_weights(j_sb)
+            group_weights(j_sb, "j_g")
             live["j"] = quantise(live["j_g"], "j_q", keep)
             for t in range(PACK):
                 leave_s(0, t, accs[t])
             leave_state(0, 0, accs[0])
             transpose_both(1)
-            do(transpose_noise, 0, 0)
             for t in range(1, PACK):
                 leave_state(0, t, accs[t])
             transpose_both(2)
             do(regroup_s, 0)
+            mask_weights(w_sb)
             do(quantise_x, 1)
             do(quantise_s, 0)
-            do(recurrent, 0, 0)
+            do(recurrent, 0, 0, 0)
+            do(recurrent, 0, 0, 1)
+            do(transpose_noise, 0, 0)
+            group_weights(w_sb, "w_g")
             project_up_to(PACK + 2)
             do(add_delta, 0, 0)
-            do(recurrent, 0, 1)
             do(add_noise, 0, 0)
-            do(transpose_noise, 0, 1)
             project_up_to(2 * PACK)
-            mask_weights(w_sb, "w_g")
+            do(recurrent, 0, 1, 0)
+            do(recurrent, 0, 1, 1)
+            do(transpose_noise, 0, 1)
             do(quantise_x, 2)
             project_up_to(2 * PACK + 2)
-            live["w"] = quantise(live["w_g"], "w_q", keep)
             do(regroup_state, 0)
+            live["w"] = quantise(live["w_g"], "w_q", keep)
             do(quantise_state, 0)
-            do(signal, 0, 0)
+            do(signal, 0, 0, 0)
             transpose_both(3)
-            project_up_to(3 * PACK)
             do(add_delta, 0, 1)
+            do(signal, 0, 0, 1)
+            do(signal, 0, 1, 0)
+            project_up_to(3 * PACK)
             do(add_noise, 0, 1)
-            do(transpose_noise, 1, 0)
+            do(signal, 0, 1, 1)
             do(regroup_s, 1)
             do(add_signal, 0, 0)
-            do(signal, 0, 1)
             do(regroup_state, 1)
             do(quantise_x, 3)
-            do(quantise_state, 1)
             do(quantise_s, 1)
-            do(regroup_s, 2)
-            do(regroup_state, 2)
-            do(recurrent, 1, 0)
+            do(quantise_state, 1)
+            do(regroup_both, 2)
+            do(recurrent, 1, 0, 0)
+            do(recurrent, 1, 0, 1)
             do(add_signal, 0, 1)
-            do(signal, 1, 0)
+            do(transpose_noise, 1, 0)
+            do(signal, 1, 0, 0)
 
-        with tc.manual_schedule(engines={mybir.EngineType.DVE, mybir.EngineType.Pool}):
             for c in range(NCH + 1):
                 half_step(c, 0)
                 half_step(c, 1)

from contextlib import ExitStack
import math

import concourse.mybir as mybir
from concourse.masks import make_identity

F32 = mybir.dt.float32
BF16 = mybir.dt.bfloat16
U32 = mybir.dt.uint32
U8 = mybir.dt.uint8
I32 = mybir.dt.int32
FP8X4 = mybir.dt.float8_e4m3fn_x4
ACT = mybir.ActivationFunctionType
ALU = mybir.AluOpType

P = 128
PACK = 4
M, D = 4096, 512
CH = 512
NCH = M // CH
SUB = CH // P
HALF = CH // 2
FLOPS = 3 * 2 * M * D * D

PI_HI = 3.1415927410125732
PI_LO = math.pi - PI_HI
SWAPPED = 1
MIXED = (NCH - 2, NCH - 1)
HALVED = (NCH - 2, NCH - 1)


def tile_brainquantumlayer_pa_t_kernel(tc, x, W_in, b_in, weights, J, theta, lam, mask, noise_raw, out):
    nc = tc.nc
    with ExitStack() as ctx:
        keep = ctx.enter_context(tc.tile_pool(name="keep", bufs=1))
        work = ctx.enter_context(tc.tile_pool(name="work", bufs=2))
        psum = ctx.enter_context(tc.psum_pool(name="psum", bufs=2))

        x_v = x.rearrange("(c p s) k -> c p s k", p=P, s=SUB)
        n_v = noise_raw.rearrange("(c p s) k -> c p s k", p=P, s=SUB)
        o_v = out.rearrange("(c p s) k -> c p s k", p=P, s=SUB)

        def load_planes(dst, w):
            rows = w.rearrange("(u p e) j -> u p (e j)", u=2, p=P, e=2)
            for u in range(2):
                nc.sync.dma_start(out=dst[:, 2 * u:2 * u + 2, :].rearrange("p e j -> p (e j)"), in_=rows[u])

        def load_vector(dst, v):
            nc.scalar.dma_start(out=dst[:].rearrange("p (u e) -> p u e", u=2),
                                in_=v.rearrange("(u p e) -> p u e", u=2, p=P, e=2))

        th_bf = keep.tile([P, PACK], BF16, name="th_bf")
        lam_bf = keep.tile([P, 1], BF16, name="lam_bf")
        with nc.allow_non_contiguous_dma(reason="one small vector, once"):
            load_vector(th_bf, theta)

        w_in_sb = keep.tile([P, PACK, D], BF16, name="w_in_sb")
        load_planes(w_in_sb, W_in)
        x_sb = [keep.tile([P, SUB, D], BF16, name="x_sb%d" % c) for c in range(NCH)]
        n_sb = [keep.tile([P, SUB, D], BF16, name="n_sb%d" % c) for c in range(NCH)]
        for h in range(2):
            nc.sync.dma_start(out=x_sb[0][:, 2 * h:2 * h + 2, :], in_=x_v[0][:, 2 * h:2 * h + 2, :])
        b_rows = keep.tile([P, P], F32, name="b_rows")
        nc.vector.memset(b_rows[:], 0.0)
        nc.sync.dma_start(out=b_rows[0:2, :].bitcast(BF16), in_=b_in.rearrange("(u w) -> u w", u=2))
        j_sb = keep.tile([P, PACK, D], BF16, name="j_sb")
        m_sb = keep.tile([P, PACK, D], BF16, name="m_sb")
        w_sb = keep.tile([P, PACK, D], BF16, name="w_sb")
        load_planes(j_sb, J)
        load_planes(m_sb, mask)
        load_planes(w_sb, weights)
        with nc.allow_non_contiguous_dma(reason="one value to each partition, once"):
            nc.sync.dma_start(out=lam_bf[:], in_=lam.partition_broadcast(P))
        for c in range(NCH):
            if c + 1 < NCH:
                nc.sync.dma_start(out=x_sb[c + 1][:], in_=x_v[c + 1])
            nc.sync.dma_start(out=n_sb[c][:], in_=n_v[c])

        ident = keep.tile([P, P], F32, name="ident")
        make_identity(nc, ident[:])

        th2 = keep.tile([P, PACK], F32, name="th2")
        nc.vector.tensor_scalar_mul(out=th2[:], in0=th_bf[:], scalar1=2.0)
        k_f = keep.tile([P, PACK], F32, name="k_f")
        nc.vector.tensor_scalar_mul(out=k_f[:], in0=th_bf[:], scalar1=2.0 / math.pi)
        k_i = keep.tile([P, PACK], I32, name="k_i")
        nc.vector.tensor_copy(out=k_i[:], in_=k_f[:])
        k_w = keep.tile([P, PACK], F32, name="k_w")
        nc.vector.tensor_copy(out=k_w[:], in_=k_i[:])
        y_hi = keep.tile([P, PACK], F32, name="y_hi")
        nc.vector.scalar_tensor_tensor(out=y_hi[:], in0=k_w[:], scalar=-PI_HI, in1=th2[:], op0=ALU.mult, op1=ALU.add)
        y = keep.tile([P, PACK], F32, name="y")
        nc.vector.scalar_tensor_tensor(out=y[:], in0=k_w[:], scalar=-PI_LO, in1=y_hi[:], op0=ALU.mult, op1=ALU.add)
        sin_y = keep.tile([P, PACK], F32, name="sin_y")
        nc.scalar.activation(out=sin_y[:], in_=y[:], func=ACT.Sin)
        first_tanh = keep.tile([P, PACK], F32, name="first_tanh")
        nc.scalar.activation(out=first_tanh[:], in_=sin_y[:], func=ACT.Tanh)
        gain = keep.tile([P, PACK], F32, name="gain")
        nc.scalar.activation(out=gain[:], in_=sin_y[:], func=ACT.Abs, scale=0.1)
        b_words = keep.tile([P, 2], F32, name="b_words")
        b_bf = b_words[:].bitcast(BF16)

        done = set()
        live = {}

        def grouped_tile():
            return work.tile([P, PACK * D], BF16, name="grouped", tag="grouped", bufs=4, align_bytes=64)

        def transpose_words(rows, h):
            bank = psum.tile([P, 2, 2 * P], F32, name="bank_w", tag="to_scalar", bufs=4)
            for i in range(2):
                words = rows[:, 2 * h + i, :].bitcast(F32)
                for v in range(2):
                    nc.tensor.transpose(out=bank[:, v, P * i:P * (i + 1)], in_=words[:, P * v:P * (v + 1)], identity=ident[:])
            return bank

        def leave_bank(bank, grouped, h, on_vector):
            dst = grouped[:].bitcast(F32).rearrange("p (m v) -> p m v", v=2)[:, 2 * P * h:2 * P * (h + 1), :]
            src = bank[:].rearrange("p v m -> p m v")
            if on_vector:
                nc.vector.tensor_copy(out=dst, in_=src)
            else:
                nc.scalar.copy(out=dst, in_=src)

        def operand_tiles(name, pool, operands=1):
            return (pool.tile([P, operands * D], U32, name=name + "_c", align_bytes=64),
                    pool.tile([P, operands * D], U8, name=name + "_s", align_bytes=64))

        def one_operand(tiles, i):
            return tiles[0][:, D * i:D * (i + 1)], tiles[1][:, D * i:D * (i + 1)]

        def quantise_into(operand, grouped):
            nc.vector.quantize_mx(out=operand[0][:].bitcast(FP8X4), scales=operand[1][:], in_=grouped[:])

        def quantise(grouped, name, pool):
            operand = operand_tiles(name, pool)
            quantise_into(operand, grouped)
            return operand

        def mx_pass(acc, stationary, t, moving, rows=slice(0, CH)):
            cols = slice(P * t, P * (t + 1))
            nc.tensor.matmul_mx(out=acc, lhsT=stationary[0][:, cols].bitcast(FP8X4), lhsT_scale=stationary[1][:, cols],
                                rhs=moving[0][:, rows].bitcast(FP8X4), rhs_scale=moving[1][:, rows], start=True, stop=True)

        def regrouped_tile(tag, operands=1):
            return work.tile([P, operands * PACK * CH], BF16, name="regrouped", tag=tag, bufs=1, align_bytes=64)

        def regroup(planes, grouped, on_vector):
            if on_vector:
                nc.vector.tensor_copy(out=grouped.rearrange("p (c i t) -> p c t i", i=4, t=PACK),
                                      in_=planes[:].rearrange("p t (c i) -> p c t i", i=4))
            else:
                nc.gpsimd.tensor_scalar(out=grouped.rearrange("p (c i t) -> p c t i", i=4, t=PACK),
                                        in0=planes[:].rearrange("p t (c i) -> p c t i", i=4),
                                        scalar1=1.0, scalar2=0.0, op0=ALU.mult, op1=ALU.add)

        def spread_b():
            bank = psum.tile([P, P], F32, name="bank_b", tag="to_scalar", bufs=4)
            nc.tensor.transpose(out=bank[:], in_=b_rows[:], identity=ident[:])
            nc.vector.tensor_copy(out=b_words[:], in_=bank[:, 0:2])

        def prepare_w_in():
            grouped = grouped_tile()
            for h in range(2):
                leave_bank(transpose_words(w_in_sb, h), grouped, h, on_vector=True)
            live["w_in_g"] = grouped

        def quantise_w_in():
            live["w_in"] = quantise(live["w_in_g"], "w_in_q", keep)

        def mask_weights(w):
            nc.vector.tensor_tensor(out=w[:], in0=w[:], in1=m_sb[:], op=ALU.mult)

        def group_weights(w, name):
            live[name] = grouped_tile()
            g_v = live[name][:].rearrange("p (u e q t) -> p u e q t", u=2, e=2, q=P, t=PACK)
            w_v = w[:].rearrange("p t (u q e) -> p u e q t", u=2, q=P, e=2)
            for e in range(2):
                nc.vector.tensor_copy(out=g_v[:, :, e, :, :], in_=w_v[:, :, e, :, :])

        def transpose_x(c, h):
            if h == 0:
                live["xg", c] = grouped_tile()
            leave_bank(transpose_words(x_sb[c], h), live["xg", c], h, on_vector=(c == 0 and h == 0))

        def quantise_x(c):
            live["xq", c] = quantise(live["xg", c], "x_q", work)

        def project(c, t):
            if t == 0:
                live["state", c] = work.tile([P, PACK, CH], BF16, name="state_pl", bufs=3)
                live["s", c] = work.tile([P, PACK, CH], F32, name="s_pl", bufs=4)
            acc = psum.tile([P, CH], F32, name="acc_state", tag="to_scalar", bufs=4)
            mx_pass(acc[:], live["w_in"], t, live["xq", c])
            leave_s(c, t, acc)
            leave_state(c, t, acc)

        def leave_s(c, t, acc):
            nc.scalar.activation(out=live["s", c][:, t, :], in_=acc[:], func=ACT.Tanh, bias=b_bf[:, t:t + 1], scale=1.0)

        def leave_state(c, t, acc):
            nc.scalar.activation(out=live["state", c][:, t, :], in_=acc[:], func=ACT.Identity, bias=b_bf[:, t:t + 1], scale=1.0)

        def project_first():
            live["state", 0] = work.tile([P, PACK, CH], BF16, name="state_pl", bufs=3)
            live["s", 0] = work.tile([P, PACK, CH], F32, name="s_pl", bufs=4)
            accs = []
            for t in range(PACK):
                acc = psum.tile([P, CH], F32, name="acc_first", tag="to_vector", bufs=4)
                mx_pass(acc[:], live["w_in"], t, live["xq", 0])
                accs.append(acc)
            for t in range(PACK):
                done.add((project, 0, (t,)))
            return accs

        def regroup_s(c):
            live["s_g", c] = regrouped_tile("state_g" if c == SWAPPED else "s_g")
            regroup(live["s", c], live["s_g", c][:], on_vector=(c == 0))

        def regroup_state(c):
            live["state_g", c] = regrouped_tile("s_g" if c == SWAPPED else "state_g")
            regroup(live["state", c], live["state_g", c][:], on_vector=True)

        def quantise_s(c):
            live["both_q", c] = operand_tiles("both_q", work, operands=2)
            live["sq", c] = one_operand(live["both_q", c], 0)
            quantise_into(live["sq", c], live["s_g", c])

        def quantise_state(c):
            live["stq", c] = one_operand(live["both_q", c], 1)
            quantise_into(live["stq", c], live["state_g", c])

        def regroup_both(c):
            live["both_g", c] = regrouped_tile("s_g", operands=2)
            for i, planes in enumerate((live["s", c], live["state", c])):
                regroup(planes, live["both_g", c][:, PACK * CH * i:PACK * CH * (i + 1)], on_vector=False)

        def quantise_both(c):
            tiles = operand_tiles("both_q", work, operands=2)
            quantise_into(tiles, live["both_g", c])
            live["sq", c], live["stq", c] = one_operand(tiles, 0), one_operand(tiles, 1)

        def half_rows(h):
            return slice(HALF * h, HALF * (h + 1))

        def product(name, c, u, v, stationary, moving):
            acc = psum.tile([P, 2, HALF], F32, name="acc_" + name, tag="to_vector", bufs=4)
            if c in HALVED:
                for e in range(2):
                    mx_pass(acc[:, e, :], stationary, 2 * v + e, moving, half_rows(u))
            else:
                mx_pass(acc[:].rearrange("p h m -> p (h m)"), stationary, 2 * u + v, moving)
            live[name, c, u, v] = acc

        def recurrent(c, u, v):
            product("rec", c, u, v, live["j"], live["sq", c])

        def signal(c, u, v):
            product("sig", c, u, v, live["w"], live["stq", c])

        def transpose_noise(c, u):
            bank = psum.tile([P, CH], F32, name="bank_n", tag="to_vector", bufs=4)
            for i in range(SUB):
                s, v = (2 * u + i % 2, i // 2) if c in HALVED else (i, u)
                nc.tensor.transpose(out=bank[:, P * i:P * (i + 1)], in_=n_sb[c][:, s, :].bitcast(F32)[:, P * v:P * (v + 1)], identity=ident[:])
            if c in MIXED:
                words = work.tile([P, CH], F32, name="noise_sb", bufs=3)
                nc.scalar.copy(out=words[:], in_=bank[:])
                bank = words
            live["noise", c, u] = bank[:].bitcast(BF16).rearrange("p (m e) -> p m e", e=2)

        def add_delta(c, u):
            if u == 0:
                live["sum", c] = work.tile([P, PACK, CH], F32, name="sum_pl", bufs=3)
            for v in range(2):
                acc = live["rec", c, u, v]
                if c in HALVED:
                    part, acc = (slice(None), slice(2 * v, 2 * v + 2), half_rows(u)), acc[:]
                else:
                    part, acc = (slice(None), 2 * u + v, slice(None)), acc[:].rearrange("p h m -> p (h m)")
                nc.vector.scalar_tensor_tensor(out=live["sum", c][part], in0=acc, scalar=lam_bf[:, 0:1],
                                               in1=live["s", c][part], op0=ALU.mult, op1=ALU.mult)

        def add_noise(c, u):
            if c in MIXED:
                return
            for e in range(2):
                t = 2 * u + e
                nc.vector.scalar_tensor_tensor(out=live["sum", c][:, t, :], in0=live["noise", c, u][:, :, e], scalar=gain[:, t:t + 1],
                                               in1=live["sum", c][:, t, :], op0=ALU.mult, op1=ALU.add)

        def add_signal(c, u):
            if c not in MIXED:
                for e in range(2):
                    t = 2 * u + e
                    nc.vector.tensor_tensor(out=live["sum", c][:, t, :], in0=live["sig", c, u, e][:].rearrange("p h m -> p (h m)"),
                                            in1=live["sum", c][:, t, :], op=ALU.add)
                return
            if u == 0:
                live["sum2", c] = work.tile([P, PACK, CH], F32, name="sum2_pl", bufs=2)
            noise = live["noise", c, u]
            for t in range(PACK) if c in HALVED else (2 * u, 2 * u + 1):
                v, e = t // 2, t % 2
                if c in HALVED:
                    out_ap, noise_ap, sig_ap = live["sum2", c][:, t, half_rows(u)], noise[:, half_rows(v), e], live["sig", c, u, v][:, e, :]
                else:
                    out_ap, noise_ap, sig_ap = live["sum2", c][:, t, :], noise[:, :, e], live["sig", c, u, e][:].rearrange("p h m -> p (h m)")
                nc.vector.scalar_tensor_tensor(out=out_ap, in0=noise_ap, scalar=gain[:, t:t + 1], in1=sig_ap, op0=ALU.mult, op1=ALU.add)

        def finish(c, s):
            if s == 0:
                live["out", c] = work.tile([P, SUB, D], F32, name="out_sb", bufs=2)
            bank = psum.tile([P, PACK, P], F32, name="bank_o", tag="to_scalar", bufs=4)
            for t in range(PACK):
                rows = slice(P * s, P * (s + 1))
                parts = [live["sum", c], live["sum2", c]] if c in MIXED else [live["sum", c]]
                for i, part in enumerate(parts):
                    nc.tensor.matmul(out=bank[:, t, :], lhsT=part[:, t, rows], rhs=ident[:], is_transpose=True,
                                     start=(i == 0), stop=(i == len(parts) - 1))
            nc.scalar.activation(out=live["out", c][:, s, :].rearrange("p (u q e) -> p u q e", u=2, q=P, e=2),
                                 in_=bank[:].rearrange("p (u e) q -> p u q e", u=2, e=2), func=ACT.Tanh)
            if c == NCH - 1:
                nc.sync.dma_start(out=o_v[c][:, s, :], in_=live["out", c][:, s, :])
            elif s == SUB - 1:
                nc.sync.dma_start(out=o_v[c], in_=live["out", c][:])

        def do(stage, c, *args):
            if 0 <= c < NCH and (stage, c, args) not in done:
                done.add((stage, c, args))
                stage(c, *args)

        def project_up_to(n):
            for i in range(min(n, PACK * NCH)):
                do(project, i // PACK, i % PACK)

        def transpose_both(c):
            do(transpose_x, c, 0)
            do(transpose_x, c, 1)

        def finish_due(c, u):
            if c - 1 not in HALVED:
                pairs = [(c - 1, u)]
            else:
                pairs = [(c - 1, 1)]
            if c in HALVED and u == 1:
                pairs.append((c, 0))
            return [(finish, chunk, 2 * pair + i) for chunk, pair in pairs for i in range(2)]

        def half_step(c, u):
            nxt = (c, 1) if u == 0 else (c + 1, 0)
            made = PACK * (c + 3) if u == 0 else PACK * (c + 3) + 2
            planes = [(project, i // PACK, i % PACK) for i in range(made - 2, made)]
            x_half = [(transpose_x, c + 4, u)]
            rows = finish_due(c, u)
            items = planes + rows + x_half if u == 0 else rows + x_half + planes
            tail = c >= NCH - 2
            early = len(rows) if tail else 0
            if tail:
                items = rows + planes + x_half
            do(add_delta, c, u)
            do(signal, c, u, 1)
            for item in items[:early]:
                do(*item)
            if u == 1:
                if c > 0:
                    do(quantise_x, c + 3)
                    do(quantise_both, c + 1)
                do(regroup_both, c + 2)
            do(recurrent, *nxt, 0)
            for item in items[early:2]:
                do(*item)
            do(add_noise, c, u)
            do(recurrent, *nxt, 1)
            for item in items[max(early, 2):4]:
                do(*item)
            do(add_signal, c, u)
            do(transpose_noise, *nxt)
            do(signal, *nxt, 0)
            for item in items[max(early, 4):]:
                do(*item)


        with tc.manual_schedule(engines={mybir.EngineType.PE, mybir.EngineType.Activation, mybir.EngineType.DVE, mybir.EngineType.Pool}):
            prepare_w_in()
            transpose_both(0)
            spread_b()
            quantise_w_in()
            do(quantise_x, 0)
            accs = project_first()
            mask_weights(j_sb)
            group_weights(j_sb, "j_g")
            live["j"] = quantise(live["j_g"], "j_q", keep)
            for t in range(PACK):
                leave_s(0, t, accs[t])
            leave_state(0, 0, accs[0])
            transpose_both(1)
            for t in range(1, PACK):
                leave_state(0, t, accs[t])
            transpose_both(2)
            do(regroup_s, 0)
            mask_weights(w_sb)
            do(quantise_x, 1)
            do(quantise_s, 0)
            do(recurrent, 0, 0, 0)
            do(recurrent, 0, 0, 1)
            do(transpose_noise, 0, 0)
            group_weights(w_sb, "w_g")
            project_up_to(PACK + 2)
            do(add_delta, 0, 0)
            do(add_noise, 0, 0)
            project_up_to(2 * PACK)
            do(recurrent, 0, 1, 0)
            do(recurrent, 0, 1, 1)
            do(transpose_noise, 0, 1)
            do(quantise_x, 2)
            project_up_to(2 * PACK + 2)
            do(regroup_state, 0)
            live["w"] = quantise(live["w_g"], "w_q", keep)
            do(quantise_state, 0)
            do(signal, 0, 0, 0)
            transpose_both(3)
            do(add_delta, 0, 1)
            do(signal, 0, 0, 1)
            do(signal, 0, 1, 0)
            project_up_to(3 * PACK)
            do(add_noise, 0, 1)
            do(signal, 0, 1, 1)
            do(regroup_s, 1)
            do(add_signal, 0, 0)
            do(regroup_state, 1)
            do(quantise_x, 3)
            do(quantise_s, 1)
            do(quantise_state, 1)
            do(regroup_both, 2)
            do(recurrent, 1, 0, 0)
            do(recurrent, 1, 0, 1)
            do(add_signal, 0, 1)
            do(transpose_noise, 1, 0)
            do(signal, 1, 0, 0)

            for c in range(NCH + 1):
                half_step(c, 0)
                half_step(c, 1)
